import numpy as np
import ml_dtypes


def mxq(x, axis, fmt="e4m3"):
    dtype, down = {"e4m3": (ml_dtypes.float8_e4m3fn, 7), "e5m2": (ml_dtypes.float8_e5m2, 14)}[fmt]
    v = np.moveaxis(np.asarray(x, np.float32).astype(ml_dtypes.bfloat16).astype(np.float64), axis, -1)
    blocks = v.reshape(v.shape[:-1] + (-1, 32))
    amax = np.abs(blocks).max(-1, keepdims=True)
    byte = np.maximum(np.where(amax > 0, np.frexp(amax)[1] - 1 + 127, 0) - down, 1)
    scale = np.exp2(byte - 127.0)
    codes = (blocks / scale).astype(np.float32).astype(dtype).astype(np.float64)
    return np.moveaxis((codes * scale).reshape(v.shape), -1, axis)


WIDE = False


def mx_kscale(k):
    if not WIDE:
        return np.ones(k)
    levels = np.array([10, -10, 5, -5, 0])
    a = np.random.permutation(np.resize(levels, k // 512 * 4)).reshape(k // 512, 4)
    idx = np.arange(k)
    return np.exp2(a[idx // 512, idx % 128 // 32])


BF16 = ml_dtypes.bfloat16


def bf(x):
    return np.asarray(x, np.float32).astype(BF16)


def f64(x):
    return np.asarray(x).astype(np.float64)


E2M1 = np.array([0.0, 0.5, 1.0, 1.5, 2.0, 3.0, 4.0, 6.0, -0.0, -0.5, -1.0, -1.5, -2.0, -3.0, -4.0, -6.0])


def pack_weight(w, fmt):
    k, n = w.shape
    w = f64(bf(w)).reshape(k // 32, 32, n)
    amax = np.abs(w).max(1)
    if fmt == "e4m3":
        byte = np.frexp(amax)[1] - 1 + 127 - 7
    else:
        mant, ex = np.frexp(amax / 6.0)
        byte = np.where(mant > 0.5, ex, ex - 1) + 127
    byte = np.clip(np.where(amax > 0, byte, 1), 1, 254)
    scaled = (w * np.exp2(127.0 - byte)[:, None, :]).reshape(k, n).astype(np.float32)
    by_word = np.ascontiguousarray(scaled.reshape(k // 512, 128, 4, n).transpose(0, 1, 3, 2))
    if fmt == "e4m3":
        words = by_word.astype(ml_dtypes.float8_e4m3fn).view(np.uint8)
    else:
        c = by_word.astype(ml_dtypes.float4_e2m1fn).view(np.uint8) & 0xF
        words = c[..., 0::2] | (c[..., 1::2] << 4)
    return np.ascontiguousarray(words), np.ascontiguousarray(byte.astype(np.uint8).reshape(k // 512, 16, n))


def unpack_weight(words, scales, fmt):
    g, p, n, _ = words.shape
    if fmt == "e4m3":
        vals = np.ascontiguousarray(words).view(ml_dtypes.float8_e4m3fn).astype(np.float64)
    else:
        nib = np.empty((g, p, n, 4), np.uint8)
        nib[..., 0::2] = words & 0xF
        nib[..., 1::2] = words >> 4
        vals = E2M1[nib]
    vals = vals * np.repeat(np.exp2(scales.astype(np.float64) - 127.0), 8, axis=1)[..., None]
    return vals.transpose(0, 1, 3, 2).reshape(g * 512, n)

def pack4(w):
    words, scales = pack_weight(w, "e2m1")
    return words.reshape(words.shape[0], 128, -1), scales


def unpack4(words, scales):
    return unpack_weight(words.reshape(words.shape[0], 128, -1, 2), scales, "e2m1")


B, T, C, D = 6, 2048, 512, 128
ROPE_BASE = 10000.0


def rotate_half(u):
    u1, u2 = np.split(u, 2, axis=-1)
    return np.concatenate([-u2, u1], axis=-1)


def rope_tables():
    inv_freq = 1.0 / (ROPE_BASE ** (f64(np.arange(0, D, 2)) / D))
    freqs = f64(np.arange(T))[:, None] * inv_freq[None, :]
    emb = np.concatenate([freqs, freqs], -1)
    return np.cos(emb), np.sin(emb)


def l2norm(u):
    return u / np.sqrt((u * u).sum(-1, keepdims=True))


def setup_inputs():
    s = mx_kscale(C)
    x = bf(np.random.standard_normal((B, T, C)) * s)
    w = np.random.standard_normal((3 * D, C)) / np.sqrt(C) / s
    words, scales = pack4(np.ascontiguousarray(w.T))
    sqk = bf(0.75 * (1.0 + 0.25 * np.random.standard_normal(D)))
    return {"x": x,
            "W_qkv_words": words,
            "W_qkv_scales": scales,
            "sqk": sqk}


def reference(x, W_qkv_words, W_qkv_scales, sqk):
    qkv = mxq(f64(x), 2, "e4m3") @ unpack4(W_qkv_words, W_qkv_scales)
    q, k, v = np.split(qkv, 3, axis=-1)
    cos, sin = rope_tables()
    q = q * cos + rotate_half(q) * sin
    k = k * cos + rotate_half(k) * sin
    g = f64(sqk)
    q = l2norm(q) * g
    k = l2norm(k) * g
    return q, k, v

@@ -1,0 +1,225 @@
+import math
+from contextlib import ExitStack
+
+import concourse.mybir as mybir
+from concourse.masks import make_identity
+
+F32 = mybir.dt.float32
+BF16 = mybir.dt.bfloat16
+I32 = mybir.dt.int32
+U32 = mybir.dt.uint32
+U8 = mybir.dt.uint8
+FP8X4 = mybir.dt.float8_e4m3fn_x4
+FP4X4 = mybir.dt.float4_e2m1fn_x4
+ALU = mybir.AluOpType
+ACT = mybir.ActivationFunctionType
+
+P = 128
+B, T, C, D = 6, 2048, 512, 128
+HALF = D // 2
+SLOTS = T // P
+GROUP = 4
+GROUPS_PER_BATCH = SLOTS // GROUP
+N_GROUPS = B * GROUPS_PER_BATCH
+PAIR = 2
+
+ROPE_BASE = 10000.0
+ROUND_MAGIC = 1.5 * 2.0**23
+
+FLOPS = 2 * B * T * C * 3 * D
+
+
+def tile_attentionhead_pa_t_kernel(tc, x, W_qkv_words, W_qkv_scales, sqk, out_0, out_1, out_2):
+    nc = tc.nc
+    x_by_slot = x.rearrange("b (p i) k -> b p i k", i=SLOTS)
+    q_by_slot = out_0.rearrange("b (p i) d -> b p i d", i=SLOTS)
+    k_by_slot = out_1.rearrange("b (p i) d -> b p i d", i=SLOTS)
+    v_by_slot = out_2.rearrange("b (p i) d -> b p i d", i=SLOTS)
+
+    with ExitStack() as ctx:
+        const = ctx.enter_context(tc.tile_pool(name="const", bufs=1))
+        x_pool = ctx.enter_context(tc.tile_pool(name="x_pool", bufs=N_GROUPS))
+        angle_pool = ctx.enter_context(tc.tile_pool(name="angle_pool", bufs=2))
+        quant_pool = ctx.enter_context(tc.tile_pool(name="quant_pool", bufs=3))
+        norm_pool = ctx.enter_context(tc.tile_pool(name="norm_pool", bufs=4))
+        prod_pool = ctx.enter_context(tc.tile_pool(name="prod_pool", bufs=3))
+        out_pool = ctx.enter_context(tc.tile_pool(name="out_pool", bufs=4))
+        psum_xt = ctx.enter_context(tc.psum_pool(name="psum_xt", bufs=2))
+        psum_qk = ctx.enter_context(tc.psum_pool(name="psum_qk", bufs=4))
+        psum_v = ctx.enter_context(tc.psum_pool(name="psum_v", bufs=2))
+
+        w_words = const.tile([P, 2 * 3 * D], U8, align_bytes=64)
+        w_scales = const.tile([P, 3 * D], U8, align_bytes=64)
+        nc.vector.memset(w_scales[:].bitcast(I32), 0)
+        nc.sync.dma_start(out=w_words[:].bitcast(I32), in_=W_qkv_words[0].bitcast(I32))
+        for quadrant in range(4):
+            nc.sync.dma_start(
+                out=w_scales[32 * quadrant : 32 * quadrant + 4, :].bitcast(I32),
+                in_=W_qkv_scales[0, 4 * quadrant : 4 * quadrant + 4, :].bitcast(I32),
+            )
+
+        x_tiles = []
+        for g in range(N_GROUPS):
+            b, first = g // GROUPS_PER_BATCH, GROUP * (g % GROUPS_PER_BATCH)
+            x_in = x_pool.tile([P, GROUP, C], BF16, name="x_in")
+            nc.sync.dma_start(out=x_in[:], in_=x_by_slot[b, :, first : first + GROUP, :])
+            x_tiles.append(x_in)
+
+        ident = const.tile([P, P], F32)
+        make_identity(nc, ident[:])
+
+        gain_bf = const.tile([P, D], BF16)
+        nc.gpsimd.dma_start(out=gain_bf[:], in_=sqk.partition_broadcast(P))
+        gains = const.tile([P, 2, D], F32)
+        nc.vector.tensor_copy(out=gains[:, 0, :], in_=gain_bf[:])
+        nc.vector.tensor_copy(out=gains[:, 1, 0:HALF], in_=gain_bf[:, HALF:D])
+        nc.vector.tensor_scalar_mul(out=gains[:, 1, HALF:D], in0=gain_bf[:, 0:HALF], scalar1=-1.0)
+
+        turns_per_token = const.tile([P, HALF], F32)
+        nc.vector.memset(turns_per_token[:, 0:1], 1.0)
+        nc.vector.tensor_scalar_mul(
+            out=turns_per_token[:, 0:1], in0=turns_per_token[:, 0:1], scalar1=1.0 / (2.0 * math.pi)
+        )
+        filled = 1
+        while filled < HALF:
+            nc.vector.tensor_scalar_mul(
+                out=turns_per_token[:, filled : 2 * filled],
+                in0=turns_per_token[:, 0:filled],
+                scalar1=ROPE_BASE ** (-filled / HALF),
+            )
+            filled *= 2
+        token_int = const.tile([P, SLOTS], I32)
+        nc.gpsimd.iota(token_int[:], pattern=[[1, SLOTS]], base=0, channel_multiplier=SLOTS)
+        token = const.tile([P, SLOTS], F32)
+        nc.vector.tensor_copy(out=token[:], in_=token_int[:])
+
+        trig = const.tile([P, SLOTS, 2, HALF], F32)
+        table = const.tile([P, SLOTS, 2, D], F32)
+        for first in range(0, SLOTS, GROUP):
+            slots = slice(first, first + GROUP)
+            turns = angle_pool.tile([P, GROUP, HALF], F32)
+            nc.vector.tensor_tensor(
+                out=turns[:],
+                in0=token[:, slots].unsqueeze(2).to_broadcast([P, GROUP, HALF]),
+                in1=turns_per_token[:].unsqueeze(1).to_broadcast([P, GROUP, HALF]),
+                op=ALU.mult,
+            )
+            whole = angle_pool.tile([P, GROUP, HALF], F32)
+            nc.vector.tensor_scalar(
+                out=whole[:], in0=turns[:], scalar1=ROUND_MAGIC, scalar2=ROUND_MAGIC, op0=ALU.add, op1=ALU.subtract
+            )
+            part = angle_pool.tile([P, GROUP, HALF], F32)
+            nc.vector.tensor_tensor(out=part[:], in0=turns[:], in1=whole[:], op=ALU.subtract)
+            quarter_minus = angle_pool.tile([P, GROUP, HALF], F32)
+            nc.vector.tensor_scalar(
+                out=quarter_minus[:], in0=part[:], scalar1=-1.0, scalar2=0.25, op0=ALU.mult, op1=ALU.add
+            )
+            folded = angle_pool.tile([P, GROUP, HALF], F32)
+            nc.vector.scalar_tensor_tensor(
+                out=folded[:], in0=part[:], scalar=0.25, in1=quarter_minus[:], op0=ALU.add, op1=ALU.min
+            )
+            nc.scalar.activation(out=trig[:, slots, 0, :], in_=folded[:], func=ACT.Sin, scale=2.0 * math.pi)
+            nc.scalar.activation(out=trig[:, slots, 1, :], in_=part[:], func=ACT.Sin, scale=2.0 * math.pi)
+            for row in range(2):
+                nc.gpsimd.tensor_tensor(
+                    out=table[:, slots, row, :].rearrange("p i (h c) -> p i h c", h=2),
+                    in0=trig[:, slots, row, :].unsqueeze(2).to_broadcast([P, GROUP, 2, HALF]),
+                    in1=gains[:, row, :]
+                    .rearrange("p (h c) -> p h c", h=2)
+                    .unsqueeze(1)
+                    .to_broadcast([P, GROUP, 2, HALF]),
+                    op=ALU.mult,
+                )
+
+        def quantise(g):
+            words_in = x_tiles[g][:].bitcast(F32)
+            grouped = quant_pool.tile([P, GROUP * C], BF16, align_bytes=64)
+            grouped_words = grouped[:].bitcast(F32).rearrange("p (s r u) -> p s r u", s=GROUP, u=2)
+            for first in range(0, GROUP, PAIR):
+                xt = psum_xt.tile([P, PAIR, 2, P], F32)
+                for s in range(PAIR):
+                    for u in range(2):
+                        nc.tensor.transpose(xt[:, s, u, :], words_in[:, first + s, u : C // 2 : 2], ident[:])
+                nc.scalar.copy(
+                    out=grouped_words[:, first : first + PAIR], in_=xt[:].rearrange("p s u r -> p s r u")
+                )
+            x_words = quant_pool.tile([P, GROUP * P], U32, align_bytes=64)
+            x_scales = quant_pool.tile([P, GROUP * P], U8, align_bytes=64)
+            nc.vector.quantize_mx(out=x_words[:].bitcast(FP8X4), scales=x_scales[:], in_=grouped[:])
+            return x_words, x_scales
+
+        def project_and_finish(g, x_words, x_scales):
+            b, first_slot = g // GROUPS_PER_BATCH, GROUP * (g % GROUPS_PER_BATCH)
+            qk_banks = [psum_qk.tile([P, PAIR, 2 * D], F32, name="qk_bank") for pair in range(GROUP // PAIR)]
+            v_bank = psum_v.tile([P, GROUP, D], F32)
+            for s in range(GROUP):
+                tokens = slice(s * P, (s + 1) * P)
+                nc.tensor.matmul_mx(
+                    out=qk_banks[s // PAIR][:, s % PAIR, :],
+                    lhsT=x_words[:, tokens].bitcast(FP8X4),
+                    lhsT_scale=x_scales[:, tokens],
+                    rhs=w_words[:, 0 : 2 * 2 * D].bitcast(FP4X4),
+                    rhs_scale=w_scales[:, 0 : 2 * D],
+                    start=True,
+                    stop=True,
+                )
+                nc.tensor.matmul_mx(
+                    out=v_bank[:, s, :],
+                    lhsT=x_words[:, tokens].bitcast(FP8X4),
+                    lhsT_scale=x_scales[:, tokens],
+                    rhs=w_words[:, 2 * 2 * D : 2 * 3 * D].bitcast(FP4X4),
+                    rhs_scale=w_scales[:, 2 * D : 3 * D],
+                    start=True,
+                    stop=True,
+                )
+
+            sum_squares = norm_pool.tile([P, GROUP * 2], F32)
+            for s in range(GROUP):
+                for o in range(2):
+                    squares = norm_pool.tile([P, D], F32)
+                    nc.scalar.activation(
+                        out=squares[:],
+                        in_=qk_banks[s // PAIR][:, s % PAIR, o * D : (o + 1) * D],
+                        func=ACT.Square,
+                        accum_out=sum_squares[:, 2 * s + o : 2 * s + o + 1],
+                    )
+            inv_norm = norm_pool.tile([P, GROUP * 2], F32)
+            nc.scalar.activation(out=inv_norm[:], in_=sum_squares[:], func=ACT.Abs_reciprocal_sqrt)
+
+            v_out = out_pool.tile([P, GROUP, D], F32)
+            nc.scalar.copy(out=v_out[:], in_=v_bank[:])
+
+            products = prod_pool.tile([P, 2, GROUP, 2, D], F32)
+            for s in range(GROUP):
+                for o in range(2):
+                    nc.vector.scalar_tensor_tensor(
+                        out=products[:, o, s, :, :],
+                        in0=qk_banks[s // PAIR][:, s % PAIR, o * D : (o + 1) * D]
+                        .unsqueeze(1)
+                        .to_broadcast([P, 2, D]),
+                        scalar=inv_norm[:, 2 * s + o : 2 * s + o + 1],
+                        in1=table[:, first_slot + s, :, :],
+                        op0=ALU.mult,
+                        op1=ALU.mult,
+                    )
+            qk_out = out_pool.tile([P, 2, GROUP, D], F32)
+            for h in range(2):
+                here = slice(h * HALF, (h + 1) * HALF)
+                other = slice((1 - h) * HALF, (2 - h) * HALF)
+                nc.gpsimd.tensor_tensor(
+                    out=qk_out[:, :, :, here],
+                    in0=products[:, :, :, 0, here],
+                    in1=products[:, :, :, 1, other],
+                    op=ALU.add,
+                )
+
+            slots = slice(first_slot, first_slot + GROUP)
+            nc.sync.dma_start(out=v_by_slot[b, :, slots, :], in_=v_out[:])
+            nc.sync.dma_start(out=q_by_slot[b, :, slots, :], in_=qk_out[:, 0])
+            nc.sync.dma_start(out=k_by_slot[b, :, slots, :], in_=qk_out[:, 1])
+
+        ready = quantise(0)
+        for g in range(N_GROUPS):
+            following = quantise(g + 1) if g + 1 < N_GROUPS else None
+            project_and_finish(g, ready[0], ready[1])
+            ready = following

@@ -45,8 +45,8 @@ def tile_attentionhead_pa_t_kernel(tc, x, W_qkv_words, W_qkv_scales, sqk, out_0,
         prod_pool = ctx.enter_context(tc.tile_pool(name="prod_pool", bufs=3))
         out_pool = ctx.enter_context(tc.tile_pool(name="out_pool", bufs=4))
         psum_xt = ctx.enter_context(tc.psum_pool(name="psum_xt", bufs=2))
-        psum_qk = ctx.enter_context(tc.psum_pool(name="psum_qk", bufs=4))
-        psum_v = ctx.enter_context(tc.psum_pool(name="psum_v", bufs=2))
+        psum_qk = ctx.enter_context(tc.psum_pool(name="psum_qk", bufs=3))
+        psum_kv = ctx.enter_context(tc.psum_pool(name="psum_kv", bufs=3))
 
         w_words = const.tile([P, 2 * 3 * D], U8, align_bytes=64)
         w_scales = const.tile([P, 3 * D], U8, align_bytes=64)
@@ -131,48 +131,35 @@ def tile_attentionhead_pa_t_kernel(tc, x, W_qkv_words, W_qkv_scales, sqk, out_0,
                     op=ALU.mult,
                 )
 
-        def quantise(g):
+        def transpose_pair(g, pair, grouped):
             words_in = x_tiles[g][:].bitcast(F32)
-            grouped = quant_pool.tile([P, GROUP * C], BF16, align_bytes=64)
             grouped_words = grouped[:].bitcast(F32).rearrange("p (s r u) -> p s r u", s=GROUP, u=2)
-            for first in range(0, GROUP, PAIR):
-                xt = psum_xt.tile([P, PAIR, 2, P], F32)
-                for s in range(PAIR):
-                    for u in range(2):
-                        nc.tensor.transpose(xt[:, s, u, :], words_in[:, first + s, u : C // 2 : 2], ident[:])
-                nc.scalar.copy(
-                    out=grouped_words[:, first : first + PAIR], in_=xt[:].rearrange("p s u r -> p s r u")
-                )
-            x_words = quant_pool.tile([P, GROUP * P], U32, align_bytes=64)
-            x_scales = quant_pool.tile([P, GROUP * P], U8, align_bytes=64)
-            nc.vector.quantize_mx(out=x_words[:].bitcast(FP8X4), scales=x_scales[:], in_=grouped[:])
-            return x_words, x_scales
+            first = pair * PAIR
+            xt = psum_xt.tile([P, PAIR, 2, P], F32)
+            for s in range(PAIR):
+                for u in range(2):
+                    nc.tensor.transpose(xt[:, s, u, :], words_in[:, first + s, u : C // 2 : 2], ident[:])
+            nc.scalar.copy(out=grouped_words[:, first : first + PAIR], in_=xt[:].rearrange("p s u r -> p s r u"))
 
-        def project_and_finish(g, x_words, x_scales):
+        def multiply_pair(pair, x_words, x_scales):
+            qk_bank = psum_qk.tile([P, PAIR, 2 * D], F32)
+            kv_bank = psum_kv.tile([P, PAIR, 2 * D], F32)
+            for s in range(PAIR):
+                tokens = slice((pair * PAIR + s) * P, (pair * PAIR + s + 1) * P)
+                for bank, first_column in ((qk_bank, 0), (kv_bank, D)):
+                    nc.tensor.matmul_mx(
+                        out=bank[:, s, :],
+                        lhsT=x_words[:, tokens].bitcast(FP8X4),
+                        lhsT_scale=x_scales[:, tokens],
+                        rhs=w_words[:, 2 * first_column : 2 * (first_column + 2 * D)].bitcast(FP4X4),
+                        rhs_scale=w_scales[:, first_column : first_column + 2 * D],
+                        start=True,
+                        stop=True,
+                    )
+            return qk_bank, kv_bank
+
+        def finish(g, qk_banks, kv_banks):
             b, first_slot = g // GROUPS_PER_BATCH, GROUP * (g % GROUPS_PER_BATCH)
-            qk_banks = [psum_qk.tile([P, PAIR, 2 * D], F32, name="qk_bank") for pair in range(GROUP // PAIR)]
-            v_bank = psum_v.tile([P, GROUP, D], F32)
-            for s in range(GROUP):
-                tokens = slice(s * P, (s + 1) * P)
-                nc.tensor.matmul_mx(
-                    out=qk_banks[s // PAIR][:, s % PAIR, :],
-                    lhsT=x_words[:, tokens].bitcast(FP8X4),
-                    lhsT_scale=x_scales[:, tokens],
-                    rhs=w_words[:, 0 : 2 * 2 * D].bitcast(FP4X4),
-                    rhs_scale=w_scales[:, 0 : 2 * D],
-                    start=True,
-                    stop=True,
-                )
-                nc.tensor.matmul_mx(
-                    out=v_bank[:, s, :],
-                    lhsT=x_words[:, tokens].bitcast(FP8X4),
-                    lhsT_scale=x_scales[:, tokens],
-                    rhs=w_words[:, 2 * 2 * D : 2 * 3 * D].bitcast(FP4X4),
-                    rhs_scale=w_scales[:, 2 * D : 3 * D],
-                    start=True,
-                    stop=True,
-                )
-
             sum_squares = norm_pool.tile([P, GROUP * 2], F32)
             for s in range(GROUP):
                 for o in range(2):
@@ -187,7 +174,8 @@ def tile_attentionhead_pa_t_kernel(tc, x, W_qkv_words, W_qkv_scales, sqk, out_0,
             nc.scalar.activation(out=inv_norm[:], in_=sum_squares[:], func=ACT.Abs_reciprocal_sqrt)
 
             v_out = out_pool.tile([P, GROUP, D], F32)
-            nc.scalar.copy(out=v_out[:], in_=v_bank[:])
+            for pair in range(GROUP // PAIR):
+                nc.scalar.copy(out=v_out[:, pair * PAIR : (pair + 1) * PAIR, :], in_=kv_banks[pair][:, :, D : 2 * D])
 
             products = prod_pool.tile([P, 2, GROUP, 2, D], F32)
             for s in range(GROUP):
@@ -218,8 +206,27 @@ def tile_attentionhead_pa_t_kernel(tc, x, W_qkv_words, W_qkv_scales, sqk, out_0,
             nc.sync.dma_start(out=q_by_slot[b, :, slots, :], in_=qk_out[:, 0])
             nc.sync.dma_start(out=k_by_slot[b, :, slots, :], in_=qk_out[:, 1])
 
-        ready = quantise(0)
-        for g in range(N_GROUPS):
-            following = quantise(g + 1) if g + 1 < N_GROUPS else None
-            project_and_finish(g, ready[0], ready[1])
-            ready = following
+        def quantise(grouped):
+            x_words = quant_pool.tile([P, GROUP * P], U32, align_bytes=64)
+            x_scales = quant_pool.tile([P, GROUP * P], U8, align_bytes=64)
+            nc.vector.quantize_mx(out=x_words[:].bitcast(FP8X4), scales=x_scales[:], in_=grouped[:])
+            return x_words, x_scales
+
+        with tc.manual_schedule(engines={mybir.EngineType.PE}):
+            ready = None
+            for g in range(-1, N_GROUPS):
+                grouped = None
+                if g + 1 < N_GROUPS:
+                    grouped = quant_pool.tile([P, GROUP * C], BF16, align_bytes=64, name="grouped")
+                qk_banks, kv_banks = [], []
+                for pair in range(GROUP // PAIR):
+                    if g + 1 < N_GROUPS:
+                        transpose_pair(g + 1, pair, grouped)
+                    if g >= 0:
+                        qk_bank, kv_bank = multiply_pair(pair, ready[0], ready[1])
+                        qk_banks.append(qk_bank)
+                        kv_banks.append(kv_bank)
+                following = quantise(grouped) if g + 1 < N_GROUPS else None
+                if g >= 0:
+                    finish(g, qk_banks, kv_banks)
+                ready = following

@@ -22,6 +22,8 @@ GROUP = 4
 GROUPS_PER_BATCH = SLOTS // GROUP
 N_GROUPS = B * GROUPS_PER_BATCH
 PAIR = 2
+PAIRS_PER_GROUP = GROUP // PAIR
+N_PAIRS = N_GROUPS * PAIRS_PER_GROUP
 
 ROPE_BASE = 10000.0
 ROUND_MAGIC = 1.5 * 2.0**23
@@ -43,10 +45,10 @@ def tile_attentionhead_pa_t_kernel(tc, x, W_qkv_words, W_qkv_scales, sqk, out_0,
         quant_pool = ctx.enter_context(tc.tile_pool(name="quant_pool", bufs=3))
         norm_pool = ctx.enter_context(tc.tile_pool(name="norm_pool", bufs=4))
         prod_pool = ctx.enter_context(tc.tile_pool(name="prod_pool", bufs=3))
-        out_pool = ctx.enter_context(tc.tile_pool(name="out_pool", bufs=4))
+        out_pool = ctx.enter_context(tc.tile_pool(name="out_pool", bufs=6))
         psum_xt = ctx.enter_context(tc.psum_pool(name="psum_xt", bufs=2))
-        psum_qk = ctx.enter_context(tc.psum_pool(name="psum_qk", bufs=3))
-        psum_kv = ctx.enter_context(tc.psum_pool(name="psum_kv", bufs=3))
+        psum_qk = ctx.enter_context(tc.psum_pool(name="psum_qk", bufs=4))
+        psum_kv = ctx.enter_context(tc.psum_pool(name="psum_kv", bufs=2))
 
         w_words = const.tile([P, 2 * 3 * D], U8, align_bytes=64)
         w_scales = const.tile([P, 3 * D], U8, align_bytes=64)
@@ -70,10 +72,11 @@ def tile_attentionhead_pa_t_kernel(tc, x, W_qkv_words, W_qkv_scales, sqk, out_0,
 
         gain_bf = const.tile([P, D], BF16)
         nc.gpsimd.dma_start(out=gain_bf[:], in_=sqk.partition_broadcast(P))
-        gains = const.tile([P, 2, D], F32)
-        nc.vector.tensor_copy(out=gains[:, 0, :], in_=gain_bf[:])
-        nc.vector.tensor_copy(out=gains[:, 1, 0:HALF], in_=gain_bf[:, HALF:D])
-        nc.vector.tensor_scalar_mul(out=gains[:, 1, HALF:D], in0=gain_bf[:, 0:HALF], scalar1=-1.0)
+        gains = const.tile([P, 2, 2, HALF], F32)
+        nc.vector.tensor_copy(out=gains[:, 0, 0, :], in_=gain_bf[:, 0:HALF])
+        nc.vector.tensor_scalar_mul(out=gains[:, 0, 1, :], in0=gain_bf[:, 0:HALF], scalar1=-1.0)
+        nc.vector.tensor_copy(out=gains[:, 1, 0, :], in_=gain_bf[:, HALF:D])
+        nc.vector.tensor_copy(out=gains[:, 1, 1, :], in_=gain_bf[:, HALF:D])
 
         turns_per_token = const.tile([P, HALF], F32)
         nc.vector.memset(turns_per_token[:, 0:1], 1.0)
@@ -93,8 +96,8 @@ def tile_attentionhead_pa_t_kernel(tc, x, W_qkv_words, W_qkv_scales, sqk, out_0,
         token = const.tile([P, SLOTS], F32)
         nc.vector.tensor_copy(out=token[:], in_=token_int[:])
 
-        trig = const.tile([P, SLOTS, 2, HALF], F32)
-        table = const.tile([P, SLOTS, 2, D], F32)
+        trig = const.tile([P, SLOTS, 3, HALF], F32)
+        table = const.tile([P, SLOTS, 2, 2, HALF], F32)
         for first in range(0, SLOTS, GROUP):
             slots = slice(first, first + GROUP)
             turns = angle_pool.tile([P, GROUP, HALF], F32)
@@ -118,34 +121,49 @@ def tile_attentionhead_pa_t_kernel(tc, x, W_qkv_words, W_qkv_scales, sqk, out_0,
             nc.vector.scalar_tensor_tensor(
                 out=folded[:], in0=part[:], scalar=0.25, in1=quarter_minus[:], op0=ALU.add, op1=ALU.min
             )
-            nc.scalar.activation(out=trig[:, slots, 0, :], in_=folded[:], func=ACT.Sin, scale=2.0 * math.pi)
+            nc.scalar.activation(
+                out=trig[:, slots, 0:3:2, :],
+                in_=folded[:].unsqueeze(2).to_broadcast([P, GROUP, 2, HALF]),
+                func=ACT.Sin,
+                scale=2.0 * math.pi,
+            )
             nc.scalar.activation(out=trig[:, slots, 1, :], in_=part[:], func=ACT.Sin, scale=2.0 * math.pi)
-            for row in range(2):
+            for h in range(2):
                 nc.gpsimd.tensor_tensor(
-                    out=table[:, slots, row, :].rearrange("p i (h c) -> p i h c", h=2),
-                    in0=trig[:, slots, row, :].unsqueeze(2).to_broadcast([P, GROUP, 2, HALF]),
-                    in1=gains[:, row, :]
-                    .rearrange("p (h c) -> p h c", h=2)
-                    .unsqueeze(1)
-                    .to_broadcast([P, GROUP, 2, HALF]),
+                    out=table[:, slots, h, :, :],
+                    in0=trig[:, slots, h : h + 2, :],
+                    in1=gains[:, h, :, :].unsqueeze(1).to_broadcast([P, GROUP, 2, HALF]),
                     op=ALU.mult,
                 )
 
-        def transpose_pair(g, pair, grouped):
+        def transpose_pair(n):
+            g, half = divmod(n, PAIRS_PER_GROUP)
             words_in = x_tiles[g][:].bitcast(F32)
-            grouped_words = grouped[:].bitcast(F32).rearrange("p (s r u) -> p s r u", s=GROUP, u=2)
-            first = pair * PAIR
-            xt = psum_xt.tile([P, PAIR, 2, P], F32)
+            xt = psum_xt.tile([P, PAIR, 2, P], F32, name="xt")
             for s in range(PAIR):
                 for u in range(2):
-                    nc.tensor.transpose(xt[:, s, u, :], words_in[:, first + s, u : C // 2 : 2], ident[:])
-            nc.scalar.copy(out=grouped_words[:, first : first + PAIR], in_=xt[:].rearrange("p s u r -> p s r u"))
+                    nc.tensor.transpose(xt[:, s, u, :], words_in[:, half * PAIR + s, u : C // 2 : 2], ident[:])
+            return xt
 
-        def multiply_pair(pair, x_words, x_scales):
-            qk_bank = psum_qk.tile([P, PAIR, 2 * D], F32)
-            kv_bank = psum_kv.tile([P, PAIR, 2 * D], F32)
+        def copy_pair(xt):
+            grouped = quant_pool.tile([P, PAIR * C], BF16, align_bytes=64, name="grouped")
+            nc.scalar.copy(
+                out=grouped[:].bitcast(F32).rearrange("p (s r u) -> p s r u", s=PAIR, u=2),
+                in_=xt[:].rearrange("p s u r -> p s r u"),
+            )
+            return grouped
+
+        def quantise_pair(grouped):
+            x_words = quant_pool.tile([P, PAIR * P], U32, align_bytes=64, name="x_words")
+            x_scales = quant_pool.tile([P, PAIR * P], U8, align_bytes=64, name="x_scales")
+            nc.vector.quantize_mx(out=x_words[:].bitcast(FP8X4), scales=x_scales[:], in_=grouped[:])
+            return x_words, x_scales
+
+        def multiply_pair(x_words, x_scales):
+            qk_bank = psum_qk.tile([P, PAIR, 2 * D], F32, name="qk_bank")
+            kv_bank = psum_kv.tile([P, PAIR, 2 * D], F32, name="kv_bank")
             for s in range(PAIR):
-                tokens = slice((pair * PAIR + s) * P, (pair * PAIR + s + 1) * P)
+                tokens = slice(s * P, (s + 1) * P)
                 for bank, first_column in ((qk_bank, 0), (kv_bank, D)):
                     nc.tensor.matmul_mx(
                         out=bank[:, s, :],
@@ -158,75 +176,77 @@ def tile_attentionhead_pa_t_kernel(tc, x, W_qkv_words, W_qkv_scales, sqk, out_0,
                     )
             return qk_bank, kv_bank
 
-        def finish(g, qk_banks, kv_banks):
-            b, first_slot = g // GROUPS_PER_BATCH, GROUP * (g % GROUPS_PER_BATCH)
-            sum_squares = norm_pool.tile([P, GROUP * 2], F32)
-            for s in range(GROUP):
+        def norms_and_v(half, qk_bank, kv_bank, v_out):
+            sum_squares = norm_pool.tile([P, PAIR * 2], F32, name="sum_squares")
+            for s in range(PAIR):
                 for o in range(2):
-                    squares = norm_pool.tile([P, D], F32)
+                    squares = norm_pool.tile([P, D], F32, name="squares")
                     nc.scalar.activation(
                         out=squares[:],
-                        in_=qk_banks[s // PAIR][:, s % PAIR, o * D : (o + 1) * D],
+                        in_=qk_bank[:, s, o * D : (o + 1) * D],
                         func=ACT.Square,
                         accum_out=sum_squares[:, 2 * s + o : 2 * s + o + 1],
                     )
-            inv_norm = norm_pool.tile([P, GROUP * 2], F32)
+            inv_norm = norm_pool.tile([P, PAIR * 2], F32, name="inv_norm")
             nc.scalar.activation(out=inv_norm[:], in_=sum_squares[:], func=ACT.Abs_reciprocal_sqrt)
+            nc.scalar.copy(out=v_out[:, half * PAIR : (half + 1) * PAIR, :], in_=kv_bank[:, :, D : 2 * D])
+            return inv_norm
 
-            v_out = out_pool.tile([P, GROUP, D], F32)
-            for pair in range(GROUP // PAIR):
-                nc.scalar.copy(out=v_out[:, pair * PAIR : (pair + 1) * PAIR, :], in_=kv_banks[pair][:, :, D : 2 * D])
-
-            products = prod_pool.tile([P, 2, GROUP, 2, D], F32)
-            for s in range(GROUP):
+        def rotate_pair(first_slot, qk_bank, inv_norm):
+            products = prod_pool.tile([P, 2, PAIR, 2, 2, HALF], F32, name="products")
+            for s in range(PAIR):
                 for o in range(2):
                     nc.vector.scalar_tensor_tensor(
-                        out=products[:, o, s, :, :],
-                        in0=qk_banks[s // PAIR][:, s % PAIR, o * D : (o + 1) * D]
-                        .unsqueeze(1)
-                        .to_broadcast([P, 2, D]),
+                        out=products[:, o, s, :, :, :].rearrange("p h j c -> p h (j c)"),
+                        in0=qk_bank[:, s, o * D : (o + 1) * D].unsqueeze(1).to_broadcast([P, 2, D]),
                         scalar=inv_norm[:, 2 * s + o : 2 * s + o + 1],
-                        in1=table[:, first_slot + s, :, :],
+                        in1=table[:, first_slot + s, :, :, :].rearrange("p h j c -> p h (j c)"),
                         op0=ALU.mult,
                         op1=ALU.mult,
                     )
-            qk_out = out_pool.tile([P, 2, GROUP, D], F32)
-            for h in range(2):
-                here = slice(h * HALF, (h + 1) * HALF)
-                other = slice((1 - h) * HALF, (2 - h) * HALF)
-                nc.gpsimd.tensor_tensor(
-                    out=qk_out[:, :, :, here],
-                    in0=products[:, :, :, 0, here],
-                    in1=products[:, :, :, 1, other],
-                    op=ALU.add,
-                )
+            return products
 
-            slots = slice(first_slot, first_slot + GROUP)
-            nc.sync.dma_start(out=v_by_slot[b, :, slots, :], in_=v_out[:])
-            nc.sync.dma_start(out=q_by_slot[b, :, slots, :], in_=qk_out[:, 0])
-            nc.sync.dma_start(out=k_by_slot[b, :, slots, :], in_=qk_out[:, 1])
+        def add_pair(half, products, qk_out):
+            terms = products[:].rearrange("p o s h j c -> p o (s h) j c")
+            nc.gpsimd.tensor_tensor(
+                out=qk_out[:, :, half * PAIR : (half + 1) * PAIR, :].rearrange("p o s (h c) -> p o (s h) c", h=2),
+                in0=terms[:, :, :, 0, :],
+                in1=terms[:, :, :, 1, :],
+                op=ALU.add,
+            )
 
-        def quantise(grouped):
-            x_words = quant_pool.tile([P, GROUP * P], U32, align_bytes=64)
-            x_scales = quant_pool.tile([P, GROUP * P], U8, align_bytes=64)
-            nc.vector.quantize_mx(out=x_words[:].bitcast(FP8X4), scales=x_scales[:], in_=grouped[:])
-            return x_words, x_scales
-
-        with tc.manual_schedule(engines={mybir.EngineType.PE}):
-            ready = None
-            for g in range(-1, N_GROUPS):
-                grouped = None
-                if g + 1 < N_GROUPS:
-                    grouped = quant_pool.tile([P, GROUP * C], BF16, align_bytes=64, name="grouped")
-                qk_banks, kv_banks = [], []
-                for pair in range(GROUP // PAIR):
-                    if g + 1 < N_GROUPS:
-                        transpose_pair(g + 1, pair, grouped)
-                    if g >= 0:
-                        qk_bank, kv_bank = multiply_pair(pair, ready[0], ready[1])
-                        qk_banks.append(qk_bank)
-                        kv_banks.append(kv_bank)
-                following = quantise(grouped) if g + 1 < N_GROUPS else None
-                if g >= 0:
-                    finish(g, qk_banks, kv_banks)
-                ready = following
+        xts, groupeds, codes, banks, inv_norms, prods = [], [], [], [], [], []
+        v_outs, qk_outs = [], []
+        with tc.manual_schedule():
+            for r in range(N_PAIRS + 7):
+                if r < N_PAIRS:
+                    xts.append(transpose_pair(r))
+                if 0 <= r - 3 < N_PAIRS:
+                    banks.append(multiply_pair(codes[r - 3][0], codes[r - 3][1]))
+                if 0 <= r - 1 < N_PAIRS:
+                    groupeds.append(copy_pair(xts[r - 1]))
+                if 0 <= r - 4 < N_PAIRS:
+                    g, half = divmod(r - 4, PAIRS_PER_GROUP)
+                    if half == 0:
+                        v_out = out_pool.tile([P, GROUP, D], F32, name="v_out")
+                        v_outs.append(v_out)
+                    inv_norms.append(norms_and_v(half, banks[r - 4][0], banks[r - 4][1], v_outs[g]))
+                    if half == PAIRS_PER_GROUP - 1:
+                        b, first_slot = g // GROUPS_PER_BATCH, GROUP * (g % GROUPS_PER_BATCH)
+                        nc.sync.dma_start(out=v_by_slot[b, :, first_slot : first_slot + GROUP, :], in_=v_outs[g][:])
+                if 0 <= r - 5 < N_PAIRS:
+                    first_slot = PAIR * ((r - 5) % (SLOTS // PAIR))
+                    prods.append(rotate_pair(first_slot, banks[r - 5][0], inv_norms[r - 5]))
+                if 0 <= r - 2 < N_PAIRS:
+                    codes.append(quantise_pair(groupeds[r - 2]))
+                if 0 <= r - 6 < N_PAIRS:
+                    g, half = divmod(r - 6, PAIRS_PER_GROUP)
+                    if half == 0:
+                        qk_out = out_pool.tile([P, 2, GROUP, D], F32, name="qk_out")
+                        qk_outs.append(qk_out)
+                    add_pair(half, prods[r - 6], qk_outs[g])
+                    if half == PAIRS_PER_GROUP - 1:
+                        b, first_slot = g // GROUPS_PER_BATCH, GROUP * (g % GROUPS_PER_BATCH)
+                        slots = slice(first_slot, first_slot + GROUP)
+                        nc.sync.dma_start(out=q_by_slot[b, :, slots, :], in_=qk_outs[g][:, 0])
+                        nc.sync.dma_start(out=k_by_slot[b, :, slots, :], in_=qk_outs[g][:, 1])

@@ -189,7 +189,10 @@ def tile_attentionhead_pa_t_kernel(tc, x, W_qkv_words, W_qkv_scales, sqk, out_0,
                     )
             inv_norm = norm_pool.tile([P, PAIR * 2], F32, name="inv_norm")
             nc.scalar.activation(out=inv_norm[:], in_=sum_squares[:], func=ACT.Abs_reciprocal_sqrt)
-            nc.scalar.copy(out=v_out[:, half * PAIR : (half + 1) * PAIR, :], in_=kv_bank[:, :, D : 2 * D])
+            if half == 0:
+                nc.scalar.copy(out=v_out[:, half * PAIR : (half + 1) * PAIR, :], in_=kv_bank[:, :, D : 2 * D])
+            else:
+                nc.vector.tensor_copy(out=v_out[:, half * PAIR : (half + 1) * PAIR, :], in_=kv_bank[:, :, D : 2 * D])
             return inv_norm
 
         def rotate_pair(first_slot, qk_bank, inv_norm):

@@ -22,8 +22,8 @@ GROUP = 4
 GROUPS_PER_BATCH = SLOTS // GROUP
 N_GROUPS = B * GROUPS_PER_BATCH
 PAIR = 2
-PAIRS_PER_GROUP = GROUP // PAIR
-N_PAIRS = N_GROUPS * PAIRS_PER_GROUP
+N_PAIRS = N_GROUPS * GROUP // PAIR
+HEAD_PAIRS = 4
 
 ROPE_BASE = 10000.0
 ROUND_MAGIC = 1.5 * 2.0**23
@@ -40,7 +40,7 @@ def tile_attentionhead_pa_t_kernel(tc, x, W_qkv_words, W_qkv_scales, sqk, out_0,
 
     with ExitStack() as ctx:
         const = ctx.enter_context(tc.tile_pool(name="const", bufs=1))
-        x_pool = ctx.enter_context(tc.tile_pool(name="x_pool", bufs=N_GROUPS))
+        x_pool = ctx.enter_context(tc.tile_pool(name="x_pool", bufs=N_GROUPS + 1))
         angle_pool = ctx.enter_context(tc.tile_pool(name="angle_pool", bufs=2))
         quant_pool = ctx.enter_context(tc.tile_pool(name="quant_pool", bufs=3))
         norm_pool = ctx.enter_context(tc.tile_pool(name="norm_pool", bufs=4))
@@ -48,41 +48,43 @@ def tile_attentionhead_pa_t_kernel(tc, x, W_qkv_words, W_qkv_scales, sqk, out_0,
         out_pool = ctx.enter_context(tc.tile_pool(name="out_pool", bufs=6))
         psum_xt = ctx.enter_context(tc.psum_pool(name="psum_xt", bufs=2))
         psum_qk = ctx.enter_context(tc.psum_pool(name="psum_qk", bufs=4))
-        psum_kv = ctx.enter_context(tc.psum_pool(name="psum_kv", bufs=2))
+        psum_v = ctx.enter_context(tc.psum_pool(name="psum_v", bufs=2))
+        ctx.enter_context(tc.manual_schedule())
 
         w_words = const.tile([P, 2 * 3 * D], U8, align_bytes=64)
         w_scales = const.tile([P, 3 * D], U8, align_bytes=64)
+        one = const.tile([P, 1], F32)
+        scratch = const.tile([P, 2], F32)
+        nc.vector.memset(one[:], 1.0)
         nc.vector.memset(w_scales[:].bitcast(I32), 0)
-        nc.sync.dma_start(out=w_words[:].bitcast(I32), in_=W_qkv_words[0].bitcast(I32))
-        for quadrant in range(4):
-            nc.sync.dma_start(
-                out=w_scales[32 * quadrant : 32 * quadrant + 4, :].bitcast(I32),
-                in_=W_qkv_scales[0, 4 * quadrant : 4 * quadrant + 4, :].bitcast(I32),
-            )
-
-        x_tiles = []
-        for g in range(N_GROUPS):
-            b, first = g // GROUPS_PER_BATCH, GROUP * (g % GROUPS_PER_BATCH)
-            x_in = x_pool.tile([P, GROUP, C], BF16, name="x_in")
-            nc.sync.dma_start(out=x_in[:], in_=x_by_slot[b, :, first : first + GROUP, :])
-            x_tiles.append(x_in)
-
+        nc.scalar.activation(out=scratch[:, 0:1], in_=one[:], func=ACT.Sin)
+        token_int = const.tile([P, SLOTS], I32)
+        nc.gpsimd.iota(token_int[:], pattern=[[1, SLOTS]], base=0, channel_multiplier=SLOTS)
         ident = const.tile([P, P], F32)
         make_identity(nc, ident[:])
 
+        x_of_pair = []
+        for g in range(N_GROUPS):
+            b, first = g // GROUPS_PER_BATCH, GROUP * (g % GROUPS_PER_BATCH)
+            pieces = (PAIR, PAIR) if g == 0 else (GROUP,)
+            for width in pieces:
+                x_in = x_pool.tile([P, width, C], BF16, name="x_in")
+                nc.sync.dma_start(out=x_in[:], in_=x_by_slot[b, :, first : first + width, :])
+                for s in range(0, width, PAIR):
+                    x_of_pair.append((x_in, s))
+                first += width
+            if g == 0:
+                nc.sync.dma_start(out=w_words[:].bitcast(I32), in_=W_qkv_words[0].bitcast(I32))
+                for quadrant in range(4):
+                    nc.sync.dma_start(
+                        out=w_scales[32 * quadrant : 32 * quadrant + 4, :].bitcast(I32),
+                        in_=W_qkv_scales[0, 4 * quadrant : 4 * quadrant + 4, :].bitcast(I32),
+                    )
         gain_bf = const.tile([P, D], BF16)
         nc.gpsimd.dma_start(out=gain_bf[:], in_=sqk.partition_broadcast(P))
-        gains = const.tile([P, 2, 2, HALF], F32)
-        nc.vector.tensor_copy(out=gains[:, 0, 0, :], in_=gain_bf[:, 0:HALF])
-        nc.vector.tensor_scalar_mul(out=gains[:, 0, 1, :], in0=gain_bf[:, 0:HALF], scalar1=-1.0)
-        nc.vector.tensor_copy(out=gains[:, 1, 0, :], in_=gain_bf[:, HALF:D])
-        nc.vector.tensor_copy(out=gains[:, 1, 1, :], in_=gain_bf[:, HALF:D])
 
         turns_per_token = const.tile([P, HALF], F32)
-        nc.vector.memset(turns_per_token[:, 0:1], 1.0)
-        nc.vector.tensor_scalar_mul(
-            out=turns_per_token[:, 0:1], in0=turns_per_token[:, 0:1], scalar1=1.0 / (2.0 * math.pi)
-        )
+        nc.vector.tensor_scalar_mul(out=turns_per_token[:, 0:1], in0=one[:], scalar1=1.0 / (2.0 * math.pi))
         filled = 1
         while filled < HALF:
             nc.vector.tensor_scalar_mul(
@@ -91,165 +93,212 @@ def tile_attentionhead_pa_t_kernel(tc, x, W_qkv_words, W_qkv_scales, sqk, out_0,
                 scalar1=ROPE_BASE ** (-filled / HALF),
             )
             filled *= 2
-        token_int = const.tile([P, SLOTS], I32)
-        nc.gpsimd.iota(token_int[:], pattern=[[1, SLOTS]], base=0, channel_multiplier=SLOTS)
         token = const.tile([P, SLOTS], F32)
         nc.vector.tensor_copy(out=token[:], in_=token_int[:])
 
-        trig = const.tile([P, SLOTS, 3, HALF], F32)
-        table = const.tile([P, SLOTS, 2, 2, HALF], F32)
+        trig = const.tile([P, SLOTS, 2, HALF], F32)
         for first in range(0, SLOTS, GROUP):
             slots = slice(first, first + GROUP)
-            turns = angle_pool.tile([P, GROUP, HALF], F32)
+            turns = angle_pool.tile([P, GROUP, HALF], F32, name="turns")
             nc.vector.tensor_tensor(
                 out=turns[:],
                 in0=token[:, slots].unsqueeze(2).to_broadcast([P, GROUP, HALF]),
                 in1=turns_per_token[:].unsqueeze(1).to_broadcast([P, GROUP, HALF]),
                 op=ALU.mult,
             )
-            whole = angle_pool.tile([P, GROUP, HALF], F32)
+            whole = angle_pool.tile([P, GROUP, HALF], F32, name="whole")
             nc.vector.tensor_scalar(
                 out=whole[:], in0=turns[:], scalar1=ROUND_MAGIC, scalar2=ROUND_MAGIC, op0=ALU.add, op1=ALU.subtract
             )
-            part = angle_pool.tile([P, GROUP, HALF], F32)
+            part = angle_pool.tile([P, GROUP, HALF], F32, name="part")
             nc.vector.tensor_tensor(out=part[:], in0=turns[:], in1=whole[:], op=ALU.subtract)
-            quarter_minus = angle_pool.tile([P, GROUP, HALF], F32)
-            nc.vector.tensor_scalar(
-                out=quarter_minus[:], in0=part[:], scalar1=-1.0, scalar2=0.25, op0=ALU.mult, op1=ALU.add
-            )
-            folded = angle_pool.tile([P, GROUP, HALF], F32)
-            nc.vector.scalar_tensor_tensor(
-                out=folded[:], in0=part[:], scalar=0.25, in1=quarter_minus[:], op0=ALU.add, op1=ALU.min
-            )
-            nc.scalar.activation(
-                out=trig[:, slots, 0:3:2, :],
-                in_=folded[:].unsqueeze(2).to_broadcast([P, GROUP, 2, HALF]),
-                func=ACT.Sin,
-                scale=2.0 * math.pi,
-            )
+            size = angle_pool.tile([P, GROUP, HALF], F32, name="size")
             nc.scalar.activation(out=trig[:, slots, 1, :], in_=part[:], func=ACT.Sin, scale=2.0 * math.pi)
-            for h in range(2):
+            nc.scalar.activation(out=size[:], in_=part[:], func=ACT.Abs)
+            nc.scalar.activation(
+                out=trig[:, slots, 0, :], in_=size[:], func=ACT.Sin, scale=-2.0 * math.pi, bias=math.pi / 2.0
+            )
+        nc.scalar.activation(out=scratch[:, 1:2], in_=one[:], func=ACT.Abs_reciprocal_sqrt)
+
+        gains = const.tile([P, 2, 2, HALF], F32)
+        nc.gpsimd.tensor_copy(out=gains[:, 0, 0, :], in_=gain_bf[:, 0:HALF])
+        nc.gpsimd.tensor_scalar(
+            out=gains[:, 0, 1, :], in0=gain_bf[:, 0:HALF], scalar1=-1.0, scalar2=0.0, op0=ALU.mult, op1=ALU.add
+        )
+        nc.gpsimd.tensor_copy(
+            out=gains[:, 1, :, :], in_=gain_bf[:, HALF:D].unsqueeze(1).to_broadcast([P, 2, HALF])
+        )
+        table = const.tile([P, SLOTS, 2, 2, HALF], F32)
+        for first in range(0, SLOTS, GROUP):
+            slots = slice(first, first + GROUP)
+            nc.gpsimd.tensor_tensor(
+                out=table[:, slots, 0, :, :],
+                in0=trig[:, slots, :, :],
+                in1=gains[:, 0, :, :].unsqueeze(1).to_broadcast([P, GROUP, 2, HALF]),
+                op=ALU.mult,
+            )
+            for j in range(2):
                 nc.gpsimd.tensor_tensor(
-                    out=table[:, slots, h, :, :],
-                    in0=trig[:, slots, h : h + 2, :],
-                    in1=gains[:, h, :, :].unsqueeze(1).to_broadcast([P, GROUP, 2, HALF]),
+                    out=table[:, slots, 1, j, :],
+                    in0=trig[:, slots, 1 - j, :],
+                    in1=gains[:, 1, j, :].unsqueeze(1).to_broadcast([P, GROUP, HALF]),
                     op=ALU.mult,
                 )
 
         def transpose_pair(n):
-            g, half = divmod(n, PAIRS_PER_GROUP)
-            words_in = x_tiles[g][:].bitcast(F32)
+            x_in, first = x_of_pair[n]
+            words_in = x_in[:].bitcast(F32)
             xt = psum_xt.tile([P, PAIR, 2, P], F32, name="xt")
             for s in range(PAIR):
                 for u in range(2):
-                    nc.tensor.transpose(xt[:, s, u, :], words_in[:, half * PAIR + s, u : C // 2 : 2], ident[:])
+                    nc.tensor.transpose(xt[:, s, u, :], words_in[:, first + s, u : C // 2 : 2], ident[:])
             return xt
 
-        def copy_pair(xt):
-            grouped = quant_pool.tile([P, PAIR * C], BF16, align_bytes=64, name="grouped")
-            nc.scalar.copy(
-                out=grouped[:].bitcast(F32).rearrange("p (s r u) -> p s r u", s=PAIR, u=2),
-                in_=xt[:].rearrange("p s u r -> p s r u"),
-            )
-            return grouped
+        def copy_pair(n, xt, grouped):
+            half = n % 2
+            out = grouped[:, half * PAIR * C : (half + 1) * PAIR * C].bitcast(F32)
+            out = out.rearrange("p (s r u) -> p s r u", s=PAIR, u=2)
+            if n < HEAD_PAIRS:
+                nc.vector.tensor_copy(out=out, in_=xt[:].rearrange("p s u r -> p s r u"))
+            else:
+                nc.scalar.copy(out=out, in_=xt[:].rearrange("p s u r -> p s r u"))
 
-        def quantise_pair(grouped):
-            x_words = quant_pool.tile([P, PAIR * P], U32, align_bytes=64, name="x_words")
-            x_scales = quant_pool.tile([P, PAIR * P], U8, align_bytes=64, name="x_scales")
+        def quantise_group(grouped):
+            x_words = quant_pool.tile([P, GROUP * P], U32, align_bytes=64, name="x_words")
+            x_scales = quant_pool.tile([P, GROUP * P], U8, align_bytes=64, name="x_scales")
             nc.vector.quantize_mx(out=x_words[:].bitcast(FP8X4), scales=x_scales[:], in_=grouped[:])
             return x_words, x_scales
 
-        def multiply_pair(x_words, x_scales):
+        def multiply_pair(n, x_words, x_scales, v_bank):
+            half = n % 2
             qk_bank = psum_qk.tile([P, PAIR, 2 * D], F32, name="qk_bank")
-            kv_bank = psum_kv.tile([P, PAIR, 2 * D], F32, name="kv_bank")
             for s in range(PAIR):
-                tokens = slice(s * P, (s + 1) * P)
-                for bank, first_column in ((qk_bank, 0), (kv_bank, D)):
-                    nc.tensor.matmul_mx(
-                        out=bank[:, s, :],
-                        lhsT=x_words[:, tokens].bitcast(FP8X4),
-                        lhsT_scale=x_scales[:, tokens],
-                        rhs=w_words[:, 2 * first_column : 2 * (first_column + 2 * D)].bitcast(FP4X4),
-                        rhs_scale=w_scales[:, first_column : first_column + 2 * D],
-                        start=True,
-                        stop=True,
-                    )
-            return qk_bank, kv_bank
+                slot = half * PAIR + s
+                tokens = slice(slot * P, (slot + 1) * P)
+                nc.tensor.matmul_mx(
+                    out=qk_bank[:, s, :],
+                    lhsT=x_words[:, tokens].bitcast(FP8X4),
+                    lhsT_scale=x_scales[:, tokens],
+                    rhs=w_words[:, 0 : 2 * 2 * D].bitcast(FP4X4),
+                    rhs_scale=w_scales[:, 0 : 2 * D],
+                    start=True,
+                    stop=True,
+                )
+                nc.tensor.matmul_mx(
+                    out=v_bank[:, slot, :],
+                    lhsT=x_words[:, tokens].bitcast(FP8X4),
+                    lhsT_scale=x_scales[:, tokens],
+                    rhs=w_words[:, 2 * 2 * D : 2 * 3 * D].bitcast(FP4X4),
+                    rhs_scale=w_scales[:, 2 * D : 3 * D],
+                    start=True,
+                    stop=True,
+                )
+            return qk_bank
 
-        def norms_and_v(half, qk_bank, kv_bank, v_out):
-            sum_squares = norm_pool.tile([P, PAIR * 2], F32, name="sum_squares")
+        def squares_pair(n, qk_bank, sum_squares):
+            half = n % 2
             for s in range(PAIR):
                 for o in range(2):
+                    column = 2 * (half * PAIR + s) + o
                     squares = norm_pool.tile([P, D], F32, name="squares")
                     nc.scalar.activation(
                         out=squares[:],
                         in_=qk_bank[:, s, o * D : (o + 1) * D],
                         func=ACT.Square,
-                        accum_out=sum_squares[:, 2 * s + o : 2 * s + o + 1],
+                        accum_out=sum_squares[:, column : column + 1],
                     )
-            inv_norm = norm_pool.tile([P, PAIR * 2], F32, name="inv_norm")
-            nc.scalar.activation(out=inv_norm[:], in_=sum_squares[:], func=ACT.Abs_reciprocal_sqrt)
-            if half == 0:
-                nc.scalar.copy(out=v_out[:, half * PAIR : (half + 1) * PAIR, :], in_=kv_bank[:, :, D : 2 * D])
-            else:
-                nc.vector.tensor_copy(out=v_out[:, half * PAIR : (half + 1) * PAIR, :], in_=kv_bank[:, :, D : 2 * D])
-            return inv_norm
 
-        def rotate_pair(first_slot, qk_bank, inv_norm):
-            products = prod_pool.tile([P, 2, PAIR, 2, 2, HALF], F32, name="products")
+        def rotate_pair(n, qk_bank, inv_norm, products):
+            half = n % 2
+            first_slot = PAIR * (n % (SLOTS // PAIR))
             for s in range(PAIR):
+                slot = half * PAIR + s
                 for o in range(2):
                     nc.vector.scalar_tensor_tensor(
-                        out=products[:, o, s, :, :, :].rearrange("p h j c -> p h (j c)"),
+                        out=products[:, o, slot, :, :, :].rearrange("p h j c -> p h (j c)"),
                         in0=qk_bank[:, s, o * D : (o + 1) * D].unsqueeze(1).to_broadcast([P, 2, D]),
-                        scalar=inv_norm[:, 2 * s + o : 2 * s + o + 1],
+                        scalar=inv_norm[:, 2 * slot + o : 2 * slot + o + 1],
                         in1=table[:, first_slot + s, :, :, :].rearrange("p h j c -> p h (j c)"),
                         op0=ALU.mult,
                         op1=ALU.mult,
                     )
-            return products
 
-        def add_pair(half, products, qk_out):
-            terms = products[:].rearrange("p o s h j c -> p o (s h) j c")
-            nc.gpsimd.tensor_tensor(
-                out=qk_out[:, :, half * PAIR : (half + 1) * PAIR, :].rearrange("p o s (h c) -> p o (s h) c", h=2),
-                in0=terms[:, :, :, 0, :],
-                in1=terms[:, :, :, 1, :],
-                op=ALU.add,
-            )
+        def place(g):
+            return g // GROUPS_PER_BATCH, GROUP * (g % GROUPS_PER_BATCH)
 
-        xts, groupeds, codes, banks, inv_norms, prods = [], [], [], [], [], []
-        v_outs, qk_outs = [], []
-        with tc.manual_schedule():
-            for r in range(N_PAIRS + 7):
-                if r < N_PAIRS:
-                    xts.append(transpose_pair(r))
-                if 0 <= r - 3 < N_PAIRS:
-                    banks.append(multiply_pair(codes[r - 3][0], codes[r - 3][1]))
-                if 0 <= r - 1 < N_PAIRS:
-                    groupeds.append(copy_pair(xts[r - 1]))
+        xts, groupeds, codes, v_banks, qk_banks = [], [], [], [], []
+        sums, inv_norms, prods, v_outs = [], [], [], []
+        for r in range(N_PAIRS + 10):
+            if r % 2 == 1 and 0 <= (r - 3) // 2 < N_GROUPS:
+                codes.append(quantise_group(groupeds[(r - 3) // 2]))
+            if 0 <= r - 1 < N_PAIRS:
+                if (r - 1) % 2 == 0:
+                    grouped = quant_pool.tile([P, GROUP * C], BF16, align_bytes=64, name="grouped")
+                    groupeds.append(grouped)
+                copy_pair(r - 1, xts[r - 1], groupeds[(r - 1) // 2])
+            if r % 2 == 0:
+                for n in (r, r + 1):
+                    if n < N_PAIRS:
+                        xts.append(transpose_pair(n))
                 if 0 <= r - 4 < N_PAIRS:
-                    g, half = divmod(r - 4, PAIRS_PER_GROUP)
-                    if half == 0:
-                        v_out = out_pool.tile([P, GROUP, D], F32, name="v_out")
-                        v_outs.append(v_out)
-                    inv_norms.append(norms_and_v(half, banks[r - 4][0], banks[r - 4][1], v_outs[g]))
-                    if half == PAIRS_PER_GROUP - 1:
-                        b, first_slot = g // GROUPS_PER_BATCH, GROUP * (g % GROUPS_PER_BATCH)
-                        nc.sync.dma_start(out=v_by_slot[b, :, first_slot : first_slot + GROUP, :], in_=v_outs[g][:])
-                if 0 <= r - 5 < N_PAIRS:
-                    first_slot = PAIR * ((r - 5) % (SLOTS // PAIR))
-                    prods.append(rotate_pair(first_slot, banks[r - 5][0], inv_norms[r - 5]))
-                if 0 <= r - 2 < N_PAIRS:
-                    codes.append(quantise_pair(groupeds[r - 2]))
-                if 0 <= r - 6 < N_PAIRS:
-                    g, half = divmod(r - 6, PAIRS_PER_GROUP)
-                    if half == 0:
-                        qk_out = out_pool.tile([P, 2, GROUP, D], F32, name="qk_out")
-                        qk_outs.append(qk_out)
-                    add_pair(half, prods[r - 6], qk_outs[g])
-                    if half == PAIRS_PER_GROUP - 1:
-                        b, first_slot = g // GROUPS_PER_BATCH, GROUP * (g % GROUPS_PER_BATCH)
-                        slots = slice(first_slot, first_slot + GROUP)
-                        nc.sync.dma_start(out=q_by_slot[b, :, slots, :], in_=qk_outs[g][:, 0])
-                        nc.sync.dma_start(out=k_by_slot[b, :, slots, :], in_=qk_outs[g][:, 1])
+                    g = (r - 4) // 2
+                    v_bank = psum_v.tile([P, GROUP, D], F32, name="v_bank")
+                    v_banks.append(v_bank)
+                    for n in (r - 4, r - 3):
+                        qk_banks.append(multiply_pair(n, codes[g][0], codes[g][1], v_bank))
+            if 0 <= r - 5 < N_PAIRS:
+                n = r - 5
+                g = n // 2
+                if n % 2 == 0:
+                    sum_squares = norm_pool.tile([P, GROUP * 2], F32, name="sum_squares")
+                    sums.append(sum_squares)
+                squares_pair(n, qk_banks[n], sums[g])
+                if n % 2 == 1:
+                    inv_norm = norm_pool.tile([P, GROUP * 2], F32, name="inv_norm")
+                    nc.scalar.activation(out=inv_norm[:], in_=sums[g][:], func=ACT.Abs_reciprocal_sqrt)
+                    inv_norms.append(inv_norm)
+                    v_out = out_pool.tile([P, GROUP, D], F32, name="v_out")
+                    v_outs.append(v_out)
+                    if g % 3 != 1:
+                        nc.scalar.copy(out=v_out[:], in_=v_banks[g][:])
+                    else:
+                        nc.vector.tensor_copy(out=v_out[:], in_=v_banks[g][:])
+                    b, first_slot = place(g)
+                    nc.sync.dma_start(out=v_by_slot[b, :, first_slot : first_slot + GROUP, :], in_=v_out[:])
+            if 0 <= r - 7 < N_PAIRS:
+                n = r - 7
+                if n % 2 == 0:
+                    products = prod_pool.tile([P, 2, GROUP, 2, 2, HALF], F32, name="products")
+                    prods.append(products)
+                rotate_pair(n, qk_banks[n], inv_norms[n // 2], prods[n // 2])
+            if r - 8 in (N_PAIRS - 2, N_PAIRS - 1):
+                half = (r - 8) % 2
+                g = N_GROUPS - 1
+                if half == 0:
+                    last_out = out_pool.tile([P, 2, GROUP, D], F32, name="qk_out")
+                mine = slice(half * PAIR, (half + 1) * PAIR)
+                terms = prods[g][:, :, mine, :, :, :].rearrange("p o s h j c -> p o (s h) j c")
+                nc.vector.tensor_tensor(
+                    out=last_out[:, :, mine, :].rearrange("p o s (h c) -> p o (s h) c", h=2),
+                    in0=terms[:, :, :, 0, :],
+                    in1=terms[:, :, :, 1, :],
+                    op=ALU.add,
+                )
+                b, first_slot = place(g)
+                slots = slice(first_slot + half * PAIR, first_slot + (half + 1) * PAIR)
+                nc.sync.dma_start(out=q_by_slot[b, :, slots, :], in_=last_out[:, 0, mine, :])
+                nc.sync.dma_start(out=k_by_slot[b, :, slots, :], in_=last_out[:, 1, mine, :])
+            if r % 2 == 1 and 0 <= (r - 9) // 2 < N_GROUPS - 1:
+                g = (r - 9) // 2
+                qk_out = out_pool.tile([P, 2, GROUP, D], F32, name="qk_out")
+                terms = prods[g][:].rearrange("p o s h j c -> p (o s h) j c")
+                nc.gpsimd.tensor_tensor(
+                    out=qk_out[:].rearrange("p o s (h c) -> p (o s h) c", h=2),
+                    in0=terms[:, :, 0, :],
+                    in1=terms[:, :, 1, :],
+                    op=ALU.add,
+                )
+                b, first_slot = place(g)
+                slots = slice(first_slot, first_slot + GROUP)
+                nc.sync.dma_start(out=q_by_slot[b, :, slots, :], in_=qk_out[:, 0])
+                nc.sync.dma_start(out=k_by_slot[b, :, slots, :], in_=qk_out[:, 1])

@@ -26,6 +26,7 @@ N_PAIRS = N_GROUPS * GROUP // PAIR
 HEAD_PAIRS = 4
 
 ROPE_BASE = 10000.0
+ROOT = 8
 ROUND_MAGIC = 1.5 * 2.0**23
 
 FLOPS = 2 * B * T * C * 3 * D
@@ -83,41 +84,62 @@ def tile_attentionhead_pa_t_kernel(tc, x, W_qkv_words, W_qkv_scales, sqk, out_0,
         gain_bf = const.tile([P, D], BF16)
         nc.gpsimd.dma_start(out=gain_bf[:], in_=sqk.partition_broadcast(P))
 
-        turns_per_token = const.tile([P, HALF], F32)
-        nc.vector.tensor_scalar_mul(out=turns_per_token[:, 0:1], in0=one[:], scalar1=1.0 / (2.0 * math.pi))
+        fine = const.tile([P, ROOT], F32)
+        coarse = const.tile([P, ROOT], F32)
+        nc.vector.tensor_scalar_mul(out=fine[:, 0:1], in0=one[:], scalar1=1.0 / (2.0 * math.pi))
+        nc.vector.tensor_copy(out=coarse[:, 0:1], in_=one[:])
         filled = 1
-        while filled < HALF:
-            nc.vector.tensor_scalar_mul(
-                out=turns_per_token[:, filled : 2 * filled],
-                in0=turns_per_token[:, 0:filled],
-                scalar1=ROPE_BASE ** (-filled / HALF),
-            )
+        while filled < ROOT:
+            for sequence, step in ((fine, 1), (coarse, ROOT)):
+                nc.vector.tensor_scalar_mul(
+                    out=sequence[:, filled : 2 * filled],
+                    in0=sequence[:, 0:filled],
+                    scalar1=ROPE_BASE ** (-filled * step / HALF),
+                )
             filled *= 2
         token = const.tile([P, SLOTS], F32)
         nc.vector.tensor_copy(out=token[:], in_=token_int[:])
+        turns_per_token = const.tile([P, HALF], F32)
+        nc.vector.tensor_tensor(
+            out=turns_per_token[:].rearrange("p (j i) -> p j i", i=ROOT),
+            in0=coarse[:].unsqueeze(2).to_broadcast([P, ROOT, ROOT]),
+            in1=fine[:].unsqueeze(1).to_broadcast([P, ROOT, ROOT]),
+            op=ALU.mult,
+        )
 
         trig = const.tile([P, SLOTS, 2, HALF], F32)
-        for first in range(0, SLOTS, GROUP):
-            slots = slice(first, first + GROUP)
-            turns = angle_pool.tile([P, GROUP, HALF], F32, name="turns")
-            nc.vector.tensor_tensor(
-                out=turns[:],
-                in0=token[:, slots].unsqueeze(2).to_broadcast([P, GROUP, HALF]),
-                in1=turns_per_token[:].unsqueeze(1).to_broadcast([P, GROUP, HALF]),
-                op=ALU.mult,
-            )
-            whole = angle_pool.tile([P, GROUP, HALF], F32, name="whole")
-            nc.vector.tensor_scalar(
-                out=whole[:], in0=turns[:], scalar1=ROUND_MAGIC, scalar2=ROUND_MAGIC, op0=ALU.add, op1=ALU.subtract
-            )
-            part = angle_pool.tile([P, GROUP, HALF], F32, name="part")
-            nc.vector.tensor_tensor(out=part[:], in0=turns[:], in1=whole[:], op=ALU.subtract)
-            size = angle_pool.tile([P, GROUP, HALF], F32, name="size")
-            nc.scalar.activation(out=trig[:, slots, 1, :], in_=part[:], func=ACT.Sin, scale=2.0 * math.pi)
-            nc.scalar.activation(out=size[:], in_=part[:], func=ACT.Abs)
-            nc.scalar.activation(
-                out=trig[:, slots, 0, :], in_=size[:], func=ACT.Sin, scale=-2.0 * math.pi, bias=math.pi / 2.0
-            )
+        for first in range(0, SLOTS, 2 * GROUP):
+            both = (slice(first, first + GROUP), slice(first + GROUP, first + 2 * GROUP))
+            turns, whole, part, size = [], [], [], []
+            for slots in both:
+                turns.append(angle_pool.tile([P, GROUP, HALF], F32, name="turns"))
+                nc.vector.tensor_tensor(
+                    out=turns[-1][:],
+                    in0=token[:, slots].unsqueeze(2).to_broadcast([P, GROUP, HALF]),
+                    in1=turns_per_token[:].unsqueeze(1).to_broadcast([P, GROUP, HALF]),
+                    op=ALU.mult,
+                )
+            for i in range(2):
+                whole.append(angle_pool.tile([P, GROUP, HALF], F32, name="whole"))
+                nc.vector.tensor_scalar(
+                    out=whole[i][:],
+                    in0=turns[i][:],
+                    scalar1=ROUND_MAGIC,
+                    scalar2=ROUND_MAGIC,
+                    op0=ALU.add,
+                    op1=ALU.subtract,
+                )
+            for i in range(2):
+                part.append(angle_pool.tile([P, GROUP, HALF], F32, name="part"))
+                nc.vector.tensor_tensor(out=part[i][:], in0=turns[i][:], in1=whole[i][:], op=ALU.subtract)
+            for i in range(2):
+                nc.scalar.activation(out=trig[:, both[i], 1, :], in_=part[i][:], func=ACT.Sin, scale=2.0 * math.pi)
+                size.append(angle_pool.tile([P, GROUP, HALF], F32, name="size"))
+                nc.scalar.activation(out=size[i][:], in_=part[i][:], func=ACT.Abs)
+            for i in range(2):
+                nc.scalar.activation(
+                    out=trig[:, both[i], 0, :], in_=size[i][:], func=ACT.Sin, scale=-2.0 * math.pi, bias=math.pi / 2.0
+                )
         nc.scalar.activation(out=scratch[:, 1:2], in_=one[:], func=ACT.Abs_reciprocal_sqrt)
 
         gains = const.tile([P, 2, 2, HALF], F32)
@@ -154,11 +176,14 @@ def tile_attentionhead_pa_t_kernel(tc, x, W_qkv_words, W_qkv_scales, sqk, out_0,
                     nc.tensor.transpose(xt[:, s, u, :], words_in[:, first + s, u : C // 2 : 2], ident[:])
             return xt
 
+        def on_vector(n):
+            return n < HEAD_PAIRS or n % 6 == 4
+
         def copy_pair(n, xt, grouped):
             half = n % 2
             out = grouped[:, half * PAIR * C : (half + 1) * PAIR * C].bitcast(F32)
             out = out.rearrange("p (s r u) -> p s r u", s=PAIR, u=2)
-            if n < HEAD_PAIRS:
+            if on_vector(n):
                 nc.vector.tensor_copy(out=out, in_=xt[:].rearrange("p s u r -> p s r u"))
             else:
                 nc.scalar.copy(out=out, in_=xt[:].rearrange("p s u r -> p s r u"))
@@ -254,15 +279,12 @@ def tile_attentionhead_pa_t_kernel(tc, x, W_qkv_words, W_qkv_scales, sqk, out_0,
                     sums.append(sum_squares)
                 squares_pair(n, qk_banks[n], sums[g])
                 if n % 2 == 1:
+                    v_out = out_pool.tile([P, GROUP, D], F32, name="v_out")
+                    v_outs.append(v_out)
+                    nc.scalar.copy(out=v_out[:], in_=v_banks[g][:])
                     inv_norm = norm_pool.tile([P, GROUP * 2], F32, name="inv_norm")
                     nc.scalar.activation(out=inv_norm[:], in_=sums[g][:], func=ACT.Abs_reciprocal_sqrt)
                     inv_norms.append(inv_norm)
-                    v_out = out_pool.tile([P, GROUP, D], F32, name="v_out")
-                    v_outs.append(v_out)
-                    if g % 3 != 1:
-                        nc.scalar.copy(out=v_out[:], in_=v_banks[g][:])
-                    else:
-                        nc.vector.tensor_copy(out=v_out[:], in_=v_banks[g][:])
                     b, first_slot = place(g)
                     nc.sync.dma_start(out=v_by_slot[b, :, first_slot : first_slot + GROUP, :], in_=v_out[:])
             if 0 <= r - 7 < N_PAIRS:

@@ -23,6 +23,7 @@ GROUPS_PER_BATCH = SLOTS // GROUP
 N_GROUPS = B * GROUPS_PER_BATCH
 PAIR = 2
 N_PAIRS = N_GROUPS * GROUP // PAIR
+AHEAD = 10
 HEAD_PAIRS = 4
 
 ROPE_BASE = 10000.0
@@ -41,12 +42,12 @@ def tile_attentionhead_pa_t_kernel(tc, x, W_qkv_words, W_qkv_scales, sqk, out_0,
 
     with ExitStack() as ctx:
         const = ctx.enter_context(tc.tile_pool(name="const", bufs=1))
-        x_pool = ctx.enter_context(tc.tile_pool(name="x_pool", bufs=N_GROUPS + 1))
+        x_pool = ctx.enter_context(tc.tile_pool(name="x_pool", bufs=AHEAD + 3))
         angle_pool = ctx.enter_context(tc.tile_pool(name="angle_pool", bufs=2))
         quant_pool = ctx.enter_context(tc.tile_pool(name="quant_pool", bufs=3))
         norm_pool = ctx.enter_context(tc.tile_pool(name="norm_pool", bufs=4))
         prod_pool = ctx.enter_context(tc.tile_pool(name="prod_pool", bufs=3))
-        out_pool = ctx.enter_context(tc.tile_pool(name="out_pool", bufs=6))
+        out_pool = ctx.enter_context(tc.tile_pool(name="out_pool", bufs=8))
         psum_xt = ctx.enter_context(tc.psum_pool(name="psum_xt", bufs=2))
         psum_qk = ctx.enter_context(tc.psum_pool(name="psum_qk", bufs=4))
         psum_v = ctx.enter_context(tc.psum_pool(name="psum_v", bufs=2))
@@ -59,13 +60,21 @@ def tile_attentionhead_pa_t_kernel(tc, x, W_qkv_words, W_qkv_scales, sqk, out_0,
         nc.vector.memset(one[:], 1.0)
         nc.vector.memset(w_scales[:].bitcast(I32), 0)
         nc.scalar.activation(out=scratch[:, 0:1], in_=one[:], func=ACT.Sin)
+        gain_rows = const.tile([P, D], BF16)
+        nc.gpsimd.memset(gain_rows[:], 0.0)
+        nc.sync.dma_start(out=gain_rows[0:1, :], in_=sqk.unsqueeze(0))
         token_int = const.tile([P, SLOTS], I32)
         nc.gpsimd.iota(token_int[:], pattern=[[1, SLOTS]], base=0, channel_multiplier=SLOTS)
+        all_ones = const.tile([P, P], BF16)
+        nc.gpsimd.memset(all_ones[:], 1.0)
         ident = const.tile([P, P], F32)
         make_identity(nc, ident[:])
+        gain_bank = psum_v.tile([P, GROUP, D], F32, name="v_bank")
+        nc.tensor.matmul(out=gain_bank[:, 0, :], lhsT=all_ones[:], rhs=gain_rows[:], start=True, stop=True)
 
         x_of_pair = []
-        for g in range(N_GROUPS):
+
+        def load_group(g):
             b, first = g // GROUPS_PER_BATCH, GROUP * (g % GROUPS_PER_BATCH)
             pieces = (PAIR, PAIR) if g == 0 else (GROUP,)
             for width in pieces:
@@ -74,15 +83,16 @@ def tile_attentionhead_pa_t_kernel(tc, x, W_qkv_words, W_qkv_scales, sqk, out_0,
                 for s in range(0, width, PAIR):
                     x_of_pair.append((x_in, s))
                 first += width
-            if g == 0:
-                nc.sync.dma_start(out=w_words[:].bitcast(I32), in_=W_qkv_words[0].bitcast(I32))
-                for quadrant in range(4):
-                    nc.sync.dma_start(
-                        out=w_scales[32 * quadrant : 32 * quadrant + 4, :].bitcast(I32),
-                        in_=W_qkv_scales[0, 4 * quadrant : 4 * quadrant + 4, :].bitcast(I32),
-                    )
-        gain_bf = const.tile([P, D], BF16)
-        nc.gpsimd.dma_start(out=gain_bf[:], in_=sqk.partition_broadcast(P))
+
+        load_group(0)
+        nc.sync.dma_start(out=w_words[:].bitcast(I32), in_=W_qkv_words[0].bitcast(I32))
+        for quadrant in range(4):
+            nc.sync.dma_start(
+                out=w_scales[32 * quadrant : 32 * quadrant + 4, :].bitcast(I32),
+                in_=W_qkv_scales[0, 4 * quadrant : 4 * quadrant + 4, :].bitcast(I32),
+            )
+        for g in range(1, AHEAD):
+            load_group(g)
 
         fine = const.tile([P, ROOT], F32)
         coarse = const.tile([P, ROOT], F32)
@@ -143,12 +153,10 @@ def tile_attentionhead_pa_t_kernel(tc, x, W_qkv_words, W_qkv_scales, sqk, out_0,
         nc.scalar.activation(out=scratch[:, 1:2], in_=one[:], func=ACT.Abs_reciprocal_sqrt)
 
         gains = const.tile([P, 2, 2, HALF], F32)
-        nc.gpsimd.tensor_copy(out=gains[:, 0, 0, :], in_=gain_bf[:, 0:HALF])
-        nc.gpsimd.tensor_scalar(
-            out=gains[:, 0, 1, :], in0=gain_bf[:, 0:HALF], scalar1=-1.0, scalar2=0.0, op0=ALU.mult, op1=ALU.add
-        )
-        nc.gpsimd.tensor_copy(
-            out=gains[:, 1, :, :], in_=gain_bf[:, HALF:D].unsqueeze(1).to_broadcast([P, 2, HALF])
+        nc.vector.tensor_copy(out=gains[:, 0, 0, :], in_=gain_bank[:, 0, 0:HALF])
+        nc.vector.tensor_scalar_mul(out=gains[:, 0, 1, :], in0=gain_bank[:, 0, 0:HALF], scalar1=-1.0)
+        nc.vector.tensor_copy(
+            out=gains[:, 1, :, :], in_=gain_bank[:, 0, HALF:D].unsqueeze(1).to_broadcast([P, 2, HALF])
         )
         table = const.tile([P, SLOTS, 2, 2, HALF], F32)
         for first in range(0, SLOTS, GROUP):
@@ -324,3 +332,5 @@ def tile_attentionhead_pa_t_kernel(tc, x, W_qkv_words, W_qkv_scales, sqk, out_0,
                 slots = slice(first_slot, first_slot + GROUP)
                 nc.sync.dma_start(out=q_by_slot[b, :, slots, :], in_=qk_out[:, 0])
                 nc.sync.dma_start(out=k_by_slot[b, :, slots, :], in_=qk_out[:, 1])
+                if g + AHEAD < N_GROUPS:
+                    load_group(g + AHEAD)

@@ -24,7 +24,7 @@ N_GROUPS = B * GROUPS_PER_BATCH
 PAIR = 2
 N_PAIRS = N_GROUPS * GROUP // PAIR
 AHEAD = 10
-HEAD_PAIRS = 4
+HEAD_PAIRS = 6
 
 ROPE_BASE = 10000.0
 ROOT = 8
@@ -85,13 +85,14 @@ def tile_attentionhead_pa_t_kernel(tc, x, W_qkv_words, W_qkv_scales, sqk, out_0,
                 first += width
 
         load_group(0)
+        load_group(1)
         nc.sync.dma_start(out=w_words[:].bitcast(I32), in_=W_qkv_words[0].bitcast(I32))
         for quadrant in range(4):
             nc.sync.dma_start(
                 out=w_scales[32 * quadrant : 32 * quadrant + 4, :].bitcast(I32),
                 in_=W_qkv_scales[0, 4 * quadrant : 4 * quadrant + 4, :].bitcast(I32),
             )
-        for g in range(1, AHEAD):
+        for g in range(2, AHEAD):
             load_group(g)
 
         fine = const.tile([P, ROOT], F32)
@@ -185,7 +186,7 @@ def tile_attentionhead_pa_t_kernel(tc, x, W_qkv_words, W_qkv_scales, sqk, out_0,
             return xt
 
         def on_vector(n):
-            return n < HEAD_PAIRS or n % 6 == 4
+            return n < HEAD_PAIRS or (n % 6 == 4 and n < N_PAIRS - 8)
 
         def copy_pair(n, xt, grouped):
             half = n % 2
@@ -270,15 +271,19 @@ def tile_attentionhead_pa_t_kernel(tc, x, W_qkv_words, W_qkv_scales, sqk, out_0,
                     groupeds.append(grouped)
                 copy_pair(r - 1, xts[r - 1], groupeds[(r - 1) // 2])
             if r % 2 == 0:
-                for n in (r, r + 1):
-                    if n < N_PAIRS:
-                        xts.append(transpose_pair(n))
+                if r != 4:
+                    for n in (r, r + 1):
+                        if n < N_PAIRS:
+                            xts.append(transpose_pair(n))
                 if 0 <= r - 4 < N_PAIRS:
                     g = (r - 4) // 2
                     v_bank = psum_v.tile([P, GROUP, D], F32, name="v_bank")
                     v_banks.append(v_bank)
                     for n in (r - 4, r - 3):
                         qk_banks.append(multiply_pair(n, codes[g][0], codes[g][1], v_bank))
+                if r == 4:
+                    for n in (r, r + 1):
+                        xts.append(transpose_pair(n))
             if 0 <= r - 5 < N_PAIRS:
                 n = r - 5
                 g = n // 2
@@ -286,13 +291,22 @@ def tile_attentionhead_pa_t_kernel(tc, x, W_qkv_words, W_qkv_scales, sqk, out_0,
                     sum_squares = norm_pool.tile([P, GROUP * 2], F32, name="sum_squares")
                     sums.append(sum_squares)
                 squares_pair(n, qk_banks[n], sums[g])
+                if g == N_GROUPS - 1:
+                    if n % 2 == 0:
+                        inv_norm = norm_pool.tile([P, GROUP * 2], F32, name="inv_norm")
+                        inv_norms.append(inv_norm)
+                    mine = slice((n % 2) * GROUP, (n % 2 + 1) * GROUP)
+                    nc.scalar.activation(
+                        out=inv_norms[g][:, mine], in_=sums[g][:, mine], func=ACT.Abs_reciprocal_sqrt
+                    )
                 if n % 2 == 1:
                     v_out = out_pool.tile([P, GROUP, D], F32, name="v_out")
                     v_outs.append(v_out)
                     nc.scalar.copy(out=v_out[:], in_=v_banks[g][:])
-                    inv_norm = norm_pool.tile([P, GROUP * 2], F32, name="inv_norm")
-                    nc.scalar.activation(out=inv_norm[:], in_=sums[g][:], func=ACT.Abs_reciprocal_sqrt)
-                    inv_norms.append(inv_norm)
+                    if g < N_GROUPS - 1:
+                        inv_norm = norm_pool.tile([P, GROUP * 2], F32, name="inv_norm")
+                        nc.scalar.activation(out=inv_norm[:], in_=sums[g][:], func=ACT.Abs_reciprocal_sqrt)
+                        inv_norms.append(inv_norm)
                     b, first_slot = place(g)
                     nc.sync.dma_start(out=v_by_slot[b, :, first_slot : first_slot + GROUP, :], in_=v_out[:])
             if 0 <= r - 7 < N_PAIRS:
@@ -301,14 +315,15 @@ def tile_attentionhead_pa_t_kernel(tc, x, W_qkv_words, W_qkv_scales, sqk, out_0,
                     products = prod_pool.tile([P, 2, GROUP, 2, 2, HALF], F32, name="products")
                     prods.append(products)
                 rotate_pair(n, qk_banks[n], inv_norms[n // 2], prods[n // 2])
-            if r - 8 in (N_PAIRS - 2, N_PAIRS - 1):
+            if N_PAIRS - 4 <= r - 8 < N_PAIRS:
                 half = (r - 8) % 2
-                g = N_GROUPS - 1
+                g = (r - 8) // 2
+                engine = nc.vector if g == N_GROUPS - 1 else nc.gpsimd
                 if half == 0:
                     last_out = out_pool.tile([P, 2, GROUP, D], F32, name="qk_out")
                 mine = slice(half * PAIR, (half + 1) * PAIR)
                 terms = prods[g][:, :, mine, :, :, :].rearrange("p o s h j c -> p o (s h) j c")
-                nc.vector.tensor_tensor(
+                engine.tensor_tensor(
                     out=last_out[:, :, mine, :].rearrange("p o s (h c) -> p o (s h) c", h=2),
                     in0=terms[:, :, :, 0, :],
                     in1=terms[:, :, :, 1, :],
@@ -318,7 +333,7 @@ def tile_attentionhead_pa_t_kernel(tc, x, W_qkv_words, W_qkv_scales, sqk, out_0,
                 slots = slice(first_slot + half * PAIR, first_slot + (half + 1) * PAIR)
                 nc.sync.dma_start(out=q_by_slot[b, :, slots, :], in_=last_out[:, 0, mine, :])
                 nc.sync.dma_start(out=k_by_slot[b, :, slots, :], in_=last_out[:, 1, mine, :])
-            if r % 2 == 1 and 0 <= (r - 9) // 2 < N_GROUPS - 1:
+            if r % 2 == 1 and 0 <= (r - 9) // 2 < N_GROUPS - 2:
                 g = (r - 9) // 2
                 qk_out = out_pool.tile([P, 2, GROUP, D], F32, name="qk_out")
                 terms = prods[g][:].rearrange("p o s h j c -> p (o s h) j c")

@@ -186,7 +186,7 @@ def tile_attentionhead_pa_t_kernel(tc, x, W_qkv_words, W_qkv_scales, sqk, out_0,
             return xt
 
         def on_vector(n):
-            return n < HEAD_PAIRS or (n % 6 == 4 and n < N_PAIRS - 8)
+            return n < HEAD_PAIRS
 
         def copy_pair(n, xt, grouped):
             half = n % 2

@@ -44,9 +44,9 @@ def tile_attentionhead_pa_t_kernel(tc, x, W_qkv_words, W_qkv_scales, sqk, out_0,
         const = ctx.enter_context(tc.tile_pool(name="const", bufs=1))
         x_pool = ctx.enter_context(tc.tile_pool(name="x_pool", bufs=AHEAD + 3))
         angle_pool = ctx.enter_context(tc.tile_pool(name="angle_pool", bufs=2))
-        quant_pool = ctx.enter_context(tc.tile_pool(name="quant_pool", bufs=3))
+        quant_pool = ctx.enter_context(tc.tile_pool(name="quant_pool", bufs=4))
         norm_pool = ctx.enter_context(tc.tile_pool(name="norm_pool", bufs=4))
-        prod_pool = ctx.enter_context(tc.tile_pool(name="prod_pool", bufs=3))
+        prod_pool = ctx.enter_context(tc.tile_pool(name="prod_pool", bufs=5))
         out_pool = ctx.enter_context(tc.tile_pool(name="out_pool", bufs=8))
         psum_xt = ctx.enter_context(tc.psum_pool(name="psum_xt", bufs=2))
         psum_qk = ctx.enter_context(tc.psum_pool(name="psum_qk", bufs=4))

@@ -53,8 +53,8 @@ def tile_attentionhead_pa_t_kernel(tc, x, W_qkv_words, W_qkv_scales, sqk, out_0,
         psum_v = ctx.enter_context(tc.psum_pool(name="psum_v", bufs=2))
         ctx.enter_context(tc.manual_schedule())
 
-        w_words = const.tile([P, 2 * 3 * D], U8, align_bytes=64)
-        w_scales = const.tile([P, 3 * D], U8, align_bytes=64)
+        w_words = const.tile([P, 2 * 4 * D], U8, align_bytes=64)
+        w_scales = const.tile([P, 4 * D], U8, align_bytes=64)
         one = const.tile([P, 1], F32)
         scratch = const.tile([P, 2], F32)
         nc.vector.memset(one[:], 1.0)
@@ -86,12 +86,14 @@ def tile_attentionhead_pa_t_kernel(tc, x, W_qkv_words, W_qkv_scales, sqk, out_0,
 
         load_group(0)
         load_group(1)
-        nc.sync.dma_start(out=w_words[:].bitcast(I32), in_=W_qkv_words[0].bitcast(I32))
+        nc.sync.dma_start(out=w_words[:, 0 : 2 * 3 * D].bitcast(I32), in_=W_qkv_words[0].bitcast(I32))
+        nc.gpsimd.tensor_copy(out=w_words[:, 2 * 3 * D :], in_=w_words[:, 0 : 2 * D])
         for quadrant in range(4):
             nc.sync.dma_start(
-                out=w_scales[32 * quadrant : 32 * quadrant + 4, :].bitcast(I32),
+                out=w_scales[32 * quadrant : 32 * quadrant + 4, 0 : 3 * D].bitcast(I32),
                 in_=W_qkv_scales[0, 4 * quadrant : 4 * quadrant + 4, :].bitcast(I32),
             )
+        nc.gpsimd.tensor_copy(out=w_scales[:, 3 * D :], in_=w_scales[:, 0:D])
         for g in range(2, AHEAD):
             load_group(g)
 
@@ -218,12 +220,13 @@ def tile_attentionhead_pa_t_kernel(tc, x, W_qkv_words, W_qkv_scales, sqk, out_0,
                     start=True,
                     stop=True,
                 )
+                width = min(2, GROUP - slot)
                 nc.tensor.matmul_mx(
-                    out=v_bank[:, slot, :],
+                    out=v_bank[:, slot : slot + width, :].rearrange("p s d -> p (s d)"),
                     lhsT=x_words[:, tokens].bitcast(FP8X4),
                     lhsT_scale=x_scales[:, tokens],
-                    rhs=w_words[:, 2 * 2 * D : 2 * 3 * D].bitcast(FP4X4),
-                    rhs_scale=w_scales[:, 2 * D : 3 * D],
+                    rhs=w_words[:, 2 * 2 * D : 2 * (2 + width) * D].bitcast(FP4X4),
+                    rhs_scale=w_scales[:, 2 * D : (2 + width) * D],
                     start=True,
                     stop=True,
                 )
@@ -271,16 +274,15 @@ def tile_attentionhead_pa_t_kernel(tc, x, W_qkv_words, W_qkv_scales, sqk, out_0,
                     groupeds.append(grouped)
                 copy_pair(r - 1, xts[r - 1], groupeds[(r - 1) // 2])
             if r % 2 == 0:
-                if r != 4:
-                    for n in (r, r + 1):
-                        if n < N_PAIRS:
-                            xts.append(transpose_pair(n))
                 if 0 <= r - 4 < N_PAIRS:
                     g = (r - 4) // 2
                     v_bank = psum_v.tile([P, GROUP, D], F32, name="v_bank")
                     v_banks.append(v_bank)
-                    for n in (r - 4, r - 3):
-                        qk_banks.append(multiply_pair(n, codes[g][0], codes[g][1], v_bank))
+                for i in range(2):
+                    if r + i < N_PAIRS and r != 4:
+                        xts.append(transpose_pair(r + i))
+                    if 0 <= r - 4 < N_PAIRS:
+                        qk_banks.append(multiply_pair(r - 4 + i, codes[g][0], codes[g][1], v_bank))
                 if r == 4:
                     for n in (r, r + 1):
                         xts.append(transpose_pair(n))

@@ -53,8 +53,8 @@ def tile_attentionhead_pa_t_kernel(tc, x, W_qkv_words, W_qkv_scales, sqk, out_0,
         psum_v = ctx.enter_context(tc.psum_pool(name="psum_v", bufs=2))
         ctx.enter_context(tc.manual_schedule())
 
-        w_words = const.tile([P, 2 * 4 * D], U8, align_bytes=64)
-        w_scales = const.tile([P, 4 * D], U8, align_bytes=64)
+        w_words = const.tile([P, 2 * 3 * D], U8, align_bytes=64)
+        w_scales = const.tile([P, 3 * D], U8, align_bytes=64)
         one = const.tile([P, 1], F32)
         scratch = const.tile([P, 2], F32)
         nc.vector.memset(one[:], 1.0)
@@ -86,14 +86,12 @@ def tile_attentionhead_pa_t_kernel(tc, x, W_qkv_words, W_qkv_scales, sqk, out_0,
 
         load_group(0)
         load_group(1)
-        nc.sync.dma_start(out=w_words[:, 0 : 2 * 3 * D].bitcast(I32), in_=W_qkv_words[0].bitcast(I32))
-        nc.gpsimd.tensor_copy(out=w_words[:, 2 * 3 * D :], in_=w_words[:, 0 : 2 * D])
+        nc.sync.dma_start(out=w_words[:].bitcast(I32), in_=W_qkv_words[0].bitcast(I32))
         for quadrant in range(4):
             nc.sync.dma_start(
-                out=w_scales[32 * quadrant : 32 * quadrant + 4, 0 : 3 * D].bitcast(I32),
+                out=w_scales[32 * quadrant : 32 * quadrant + 4, :].bitcast(I32),
                 in_=W_qkv_scales[0, 4 * quadrant : 4 * quadrant + 4, :].bitcast(I32),
             )
-        nc.gpsimd.tensor_copy(out=w_scales[:, 3 * D :], in_=w_scales[:, 0:D])
         for g in range(2, AHEAD):
             load_group(g)
 
@@ -221,12 +219,13 @@ def tile_attentionhead_pa_t_kernel(tc, x, W_qkv_words, W_qkv_scales, sqk, out_0,
                     stop=True,
                 )
                 width = min(2, GROUP - slot)
+                end = GROUP - slot
                 nc.tensor.matmul_mx(
-                    out=v_bank[:, slot : slot + width, :].rearrange("p s d -> p (s d)"),
+                    out=v_bank[:, end - width : end, :].rearrange("p s d -> p (s d)"),
                     lhsT=x_words[:, tokens].bitcast(FP8X4),
                     lhsT_scale=x_scales[:, tokens],
-                    rhs=w_words[:, 2 * 2 * D : 2 * (2 + width) * D].bitcast(FP4X4),
-                    rhs_scale=w_scales[:, 2 * D : (2 + width) * D],
+                    rhs=w_words[:, 2 * (3 - width) * D : 2 * 3 * D].bitcast(FP4X4),
+                    rhs_scale=w_scales[:, (3 - width) * D : 3 * D],
                     start=True,
                     stop=True,
                 )
@@ -304,7 +303,7 @@ def tile_attentionhead_pa_t_kernel(tc, x, W_qkv_words, W_qkv_scales, sqk, out_0,
                 if n % 2 == 1:
                     v_out = out_pool.tile([P, GROUP, D], F32, name="v_out")
                     v_outs.append(v_out)
-                    nc.scalar.copy(out=v_out[:], in_=v_banks[g][:])
+                    nc.scalar.copy(out=v_out[:], in_=v_banks[g][:, ::-1, :])
                     if g < N_GROUPS - 1:
                         inv_norm = norm_pool.tile([P, GROUP * 2], F32, name="inv_norm")
                         nc.scalar.activation(out=inv_norm[:], in_=sums[g][:], func=ACT.Abs_reciprocal_sqrt)

@@ -63,14 +63,17 @@ def tile_attentionhead_pa_t_kernel(tc, x, W_qkv_words, W_qkv_scales, sqk, out_0,
         gain_rows = const.tile([P, D], BF16)
         nc.gpsimd.memset(gain_rows[:], 0.0)
         nc.sync.dma_start(out=gain_rows[0:1, :], in_=sqk.unsqueeze(0))
+        minus_ones = const.tile([P, P], BF16)
         token_int = const.tile([P, SLOTS], I32)
         nc.gpsimd.iota(token_int[:], pattern=[[1, SLOTS]], base=0, channel_multiplier=SLOTS)
         all_ones = const.tile([P, P], BF16)
         nc.gpsimd.memset(all_ones[:], 1.0)
+        nc.gpsimd.memset(minus_ones[:], -1.0)
         ident = const.tile([P, P], F32)
         make_identity(nc, ident[:])
         gain_bank = psum_v.tile([P, GROUP, D], F32, name="v_bank")
         nc.tensor.matmul(out=gain_bank[:, 0, :], lhsT=all_ones[:], rhs=gain_rows[:], start=True, stop=True)
+        nc.tensor.matmul(out=gain_bank[:, 1, :], lhsT=minus_ones[:], rhs=gain_rows[:], start=True, stop=True)
 
         x_of_pair = []
 
@@ -154,27 +157,30 @@ def tile_attentionhead_pa_t_kernel(tc, x, W_qkv_words, W_qkv_scales, sqk, out_0,
         nc.scalar.activation(out=scratch[:, 1:2], in_=one[:], func=ACT.Abs_reciprocal_sqrt)
 
         gains = const.tile([P, 2, 2, HALF], F32)
-        nc.vector.tensor_copy(out=gains[:, 0, 0, :], in_=gain_bank[:, 0, 0:HALF])
-        nc.vector.tensor_scalar_mul(out=gains[:, 0, 1, :], in0=gain_bank[:, 0, 0:HALF], scalar1=-1.0)
-        nc.vector.tensor_copy(
-            out=gains[:, 1, :, :], in_=gain_bank[:, 0, HALF:D].unsqueeze(1).to_broadcast([P, 2, HALF])
-        )
+        signed_first = gain_bank[:, 0:2, 0:HALF]
+        second = gain_bank[:, 0, HALF:D]
+        nc.vector.tensor_copy(out=gains[:, 0, :, :], in_=signed_first)
+        nc.vector.tensor_copy(out=gains[:, 1, :, :], in_=second.unsqueeze(1).to_broadcast([P, 2, HALF]))
         table = const.tile([P, SLOTS, 2, 2, HALF], F32)
-        for first in range(0, SLOTS, GROUP):
-            slots = slice(first, first + GROUP)
-            nc.gpsimd.tensor_tensor(
+
+        def build_table(engine, block, signed_pair, other):
+            slots = slice(block * GROUP, (block + 1) * GROUP)
+            engine.tensor_tensor(
                 out=table[:, slots, 0, :, :],
                 in0=trig[:, slots, :, :],
-                in1=gains[:, 0, :, :].unsqueeze(1).to_broadcast([P, GROUP, 2, HALF]),
+                in1=signed_pair.unsqueeze(1).to_broadcast([P, GROUP, 2, HALF]),
                 op=ALU.mult,
             )
             for j in range(2):
-                nc.gpsimd.tensor_tensor(
+                engine.tensor_tensor(
                     out=table[:, slots, 1, j, :],
                     in0=trig[:, slots, 1 - j, :],
-                    in1=gains[:, 1, j, :].unsqueeze(1).to_broadcast([P, GROUP, HALF]),
+                    in1=other.unsqueeze(1).to_broadcast([P, GROUP, HALF]),
                     op=ALU.mult,
                 )
+
+        for block in range(1, GROUPS_PER_BATCH):
+            build_table(nc.gpsimd, block, gains[:, 0, :, :], gains[:, 1, 0, :])
 
         def transpose_pair(n):
             x_in, first = x_of_pair[n]
@@ -265,6 +271,8 @@ def tile_attentionhead_pa_t_kernel(tc, x, W_qkv_words, W_qkv_scales, sqk, out_0,
         xts, groupeds, codes, v_banks, qk_banks = [], [], [], [], []
         sums, inv_norms, prods, v_outs = [], [], [], []
         for r in range(N_PAIRS + 10):
+            if r == 4:
+                build_table(nc.vector, 0, signed_first, second)
             if r % 2 == 1 and 0 <= (r - 3) // 2 < N_GROUPS:
                 codes.append(quantise_group(groupeds[(r - 3) // 2]))
             if 0 <= r - 1 < N_PAIRS:

@@ -73,7 +73,8 @@ def tile_attentionhead_pa_t_kernel(tc, x, W_qkv_words, W_qkv_scales, sqk, out_0,
         make_identity(nc, ident[:])
         gain_bank = psum_v.tile([P, GROUP, D], F32, name="v_bank")
         nc.tensor.matmul(out=gain_bank[:, 0, :], lhsT=all_ones[:], rhs=gain_rows[:], start=True, stop=True)
-        nc.tensor.matmul(out=gain_bank[:, 1, :], lhsT=minus_ones[:], rhs=gain_rows[:], start=True, stop=True)
+        nc.tensor.matmul(out=gain_bank[:, 1, 0:HALF], lhsT=all_ones[:], rhs=gain_rows[:, HALF:D], start=True, stop=True)
+        nc.tensor.matmul(out=gain_bank[:, 1, HALF:D], lhsT=minus_ones[:], rhs=gain_rows[:, 0:HALF], start=True, stop=True)
 
         x_of_pair = []
 
@@ -156,31 +157,24 @@ def tile_attentionhead_pa_t_kernel(tc, x, W_qkv_words, W_qkv_scales, sqk, out_0,
                 )
         nc.scalar.activation(out=scratch[:, 1:2], in_=one[:], func=ACT.Abs_reciprocal_sqrt)
 
-        gains = const.tile([P, 2, 2, HALF], F32)
-        signed_first = gain_bank[:, 0:2, 0:HALF]
-        second = gain_bank[:, 0, HALF:D]
-        nc.vector.tensor_copy(out=gains[:, 0, :, :], in_=signed_first)
-        nc.vector.tensor_copy(out=gains[:, 1, :, :], in_=second.unsqueeze(1).to_broadcast([P, 2, HALF]))
-        table = const.tile([P, SLOTS, 2, 2, HALF], F32)
+        gains = const.tile([P, 2, D], F32)
+        nc.vector.tensor_copy(out=gains[:], in_=gain_bank[:, 0:2, :])
+        table = const.tile([P, SLOTS, 2, D], F32)
 
-        def build_table(engine, block, signed_pair, other):
+        def build_table(engine, block, gain_pair):
             slots = slice(block * GROUP, (block + 1) * GROUP)
-            engine.tensor_tensor(
-                out=table[:, slots, 0, :, :],
-                in0=trig[:, slots, :, :],
-                in1=signed_pair.unsqueeze(1).to_broadcast([P, GROUP, 2, HALF]),
-                op=ALU.mult,
-            )
-            for j in range(2):
+            for a in range(2):
                 engine.tensor_tensor(
-                    out=table[:, slots, 1, j, :],
-                    in0=trig[:, slots, 1 - j, :],
-                    in1=other.unsqueeze(1).to_broadcast([P, GROUP, HALF]),
+                    out=table[:, slots, a, :].rearrange("p s (j c) -> p s j c", j=2),
+                    in0=trig[:, slots, a, :].unsqueeze(2).to_broadcast([P, GROUP, 2, HALF]),
+                    in1=gain_pair[:, a, :].rearrange("p (j c) -> p j c", j=2).unsqueeze(1).to_broadcast(
+                        [P, GROUP, 2, HALF]
+                    ),
                     op=ALU.mult,
                 )
 
         for block in range(1, GROUPS_PER_BATCH):
-            build_table(nc.gpsimd, block, gains[:, 0, :, :], gains[:, 1, 0, :])
+            build_table(nc.gpsimd, block, gains)
 
         def transpose_pair(n):
             x_in, first = x_of_pair[n]
@@ -257,10 +251,10 @@ def tile_attentionhead_pa_t_kernel(tc, x, W_qkv_words, W_qkv_scales, sqk, out_0,
                 slot = half * PAIR + s
                 for o in range(2):
                     nc.vector.scalar_tensor_tensor(
-                        out=products[:, o, slot, :, :, :].rearrange("p h j c -> p h (j c)"),
+                        out=products[:, :, o, slot, :],
                         in0=qk_bank[:, s, o * D : (o + 1) * D].unsqueeze(1).to_broadcast([P, 2, D]),
                         scalar=inv_norm[:, 2 * slot + o : 2 * slot + o + 1],
-                        in1=table[:, first_slot + s, :, :, :].rearrange("p h j c -> p h (j c)"),
+                        in1=table[:, first_slot + s, :, :],
                         op0=ALU.mult,
                         op1=ALU.mult,
                     )
@@ -272,7 +266,7 @@ def tile_attentionhead_pa_t_kernel(tc, x, W_qkv_words, W_qkv_scales, sqk, out_0,
         sums, inv_norms, prods, v_outs = [], [], [], []
         for r in range(N_PAIRS + 10):
             if r == 4:
-                build_table(nc.vector, 0, signed_first, second)
+                build_table(nc.vector, 0, gain_bank)
             if r % 2 == 1 and 0 <= (r - 3) // 2 < N_GROUPS:
                 codes.append(quantise_group(groupeds[(r - 3) // 2]))
             if 0 <= r - 1 < N_PAIRS:
@@ -321,23 +315,24 @@ def tile_attentionhead_pa_t_kernel(tc, x, W_qkv_words, W_qkv_scales, sqk, out_0,
             if 0 <= r - 7 < N_PAIRS:
                 n = r - 7
                 if n % 2 == 0:
-                    products = prod_pool.tile([P, 2, GROUP, 2, 2, HALF], F32, name="products")
+                    products = prod_pool.tile([P, 2, 2, GROUP, D], F32, name="products")
                     prods.append(products)
                 rotate_pair(n, qk_banks[n], inv_norms[n // 2], prods[n // 2])
             if N_PAIRS - 4 <= r - 8 < N_PAIRS:
                 half = (r - 8) % 2
                 g = (r - 8) // 2
-                engine = nc.vector if g == N_GROUPS - 1 else nc.gpsimd
+                engine = nc.vector if g == N_GROUPS - 1 or half == 0 else nc.gpsimd
                 if half == 0:
                     last_out = out_pool.tile([P, 2, GROUP, D], F32, name="qk_out")
                 mine = slice(half * PAIR, (half + 1) * PAIR)
-                terms = prods[g][:, :, mine, :, :, :].rearrange("p o s h j c -> p o (s h) j c")
-                engine.tensor_tensor(
-                    out=last_out[:, :, mine, :].rearrange("p o s (h c) -> p o (s h) c", h=2),
-                    in0=terms[:, :, :, 0, :],
-                    in1=terms[:, :, :, 1, :],
-                    op=ALU.add,
-                )
+                for o in range(2):
+                    terms = prods[g][:, :, o, mine, :].rearrange("p a s (h c) -> p a s h c", h=2)
+                    engine.tensor_tensor(
+                        out=last_out[:, o, mine, :].rearrange("p s (h c) -> p s h c", h=2),
+                        in0=terms[:, 0],
+                        in1=terms[:, 1, :, ::-1, :],
+                        op=ALU.add,
+                    )
                 b, first_slot = place(g)
                 slots = slice(first_slot + half * PAIR, first_slot + (half + 1) * PAIR)
                 nc.sync.dma_start(out=q_by_slot[b, :, slots, :], in_=last_out[:, 0, mine, :])
@@ -345,11 +340,11 @@ def tile_attentionhead_pa_t_kernel(tc, x, W_qkv_words, W_qkv_scales, sqk, out_0,
             if r % 2 == 1 and 0 <= (r - 9) // 2 < N_GROUPS - 2:
                 g = (r - 9) // 2
                 qk_out = out_pool.tile([P, 2, GROUP, D], F32, name="qk_out")
-                terms = prods[g][:].rearrange("p o s h j c -> p (o s h) j c")
+                terms = prods[g][:].rearrange("p a o s (h c) -> p a (o s) h c", h=2)
                 nc.gpsimd.tensor_tensor(
-                    out=qk_out[:].rearrange("p o s (h c) -> p (o s h) c", h=2),
-                    in0=terms[:, :, 0, :],
-                    in1=terms[:, :, 1, :],
+                    out=qk_out[:].rearrange("p o s (h c) -> p (o s) h c", h=2),
+                    in0=terms[:, 0],
+                    in1=terms[:, 1, :, ::-1, :],
                     op=ALU.add,
                 )
                 b, first_slot = place(g)

import math
from contextlib import ExitStack

import concourse.mybir as mybir
from concourse.masks import make_identity

F32 = mybir.dt.float32
BF16 = mybir.dt.bfloat16
I32 = mybir.dt.int32
U32 = mybir.dt.uint32
U8 = mybir.dt.uint8
FP8X4 = mybir.dt.float8_e4m3fn_x4
FP4X4 = mybir.dt.float4_e2m1fn_x4
ALU = mybir.AluOpType
ACT = mybir.ActivationFunctionType

P = 128
B, T, C, D = 6, 2048, 512, 128
HALF = D // 2
SLOTS = T // P
GROUP = 4
GROUPS_PER_BATCH = SLOTS // GROUP
N_GROUPS = B * GROUPS_PER_BATCH
PAIR = 2
N_PAIRS = N_GROUPS * GROUP // PAIR
AHEAD = 10
HEAD_PAIRS = 6

ROPE_BASE = 10000.0
ROOT = 8
ROUND_MAGIC = 1.5 * 2.0**23

FLOPS = 2 * B * T * C * 3 * D


def tile_attentionhead_pa_t_kernel(tc, x, W_qkv_words, W_qkv_scales, sqk, out_0, out_1, out_2):
    nc = tc.nc
    x_by_slot = x.rearrange("b (p i) k -> b p i k", i=SLOTS)
    q_by_slot = out_0.rearrange("b (p i) d -> b p i d", i=SLOTS)
    k_by_slot = out_1.rearrange("b (p i) d -> b p i d", i=SLOTS)
    v_by_slot = out_2.rearrange("b (p i) d -> b p i d", i=SLOTS)

    with ExitStack() as ctx:
        const = ctx.enter_context(tc.tile_pool(name="const", bufs=1))
        x_pool = ctx.enter_context(tc.tile_pool(name="x_pool", bufs=AHEAD + 3))
        angle_pool = ctx.enter_context(tc.tile_pool(name="angle_pool", bufs=2))
        quant_pool = ctx.enter_context(tc.tile_pool(name="quant_pool", bufs=4))
        norm_pool = ctx.enter_context(tc.tile_pool(name="norm_pool", bufs=4))
        prod_pool = ctx.enter_context(tc.tile_pool(name="prod_pool", bufs=5))
        out_pool = ctx.enter_context(tc.tile_pool(name="out_pool", bufs=8))
        psum_xt = ctx.enter_context(tc.psum_pool(name="psum_xt", bufs=2))
        psum_qk = ctx.enter_context(tc.psum_pool(name="psum_qk", bufs=4))
        psum_v = ctx.enter_context(tc.psum_pool(name="psum_v", bufs=2))
        ctx.enter_context(tc.manual_schedule())

        w_words = const.tile([P, 2 * 3 * D], U8, align_bytes=64)
        w_scales = const.tile([P, 3 * D], U8, align_bytes=64)
        one = const.tile([P, 1], F32)
        scratch = const.tile([P, 2], F32)
        nc.vector.memset(one[:], 1.0)
        nc.vector.memset(w_scales[:].bitcast(I32), 0)
        nc.scalar.activation(out=scratch[:, 0:1], in_=one[:], func=ACT.Sin)
        gain_rows = const.tile([P, D], BF16)
        nc.gpsimd.memset(gain_rows[:], 0.0)
        nc.sync.dma_start(out=gain_rows[0:1, :], in_=sqk.unsqueeze(0))
        minus_ones = const.tile([P, P], BF16)
        token_int = const.tile([P, SLOTS], I32)
        nc.gpsimd.iota(token_int[:], pattern=[[1, SLOTS]], base=0, channel_multiplier=SLOTS)
        all_ones = const.tile([P, P], BF16)
        nc.gpsimd.memset(all_ones[:], 1.0)
        nc.gpsimd.memset(minus_ones[:], -1.0)
        ident = const.tile([P, P], F32)
        make_identity(nc, ident[:])
        gain_bank = psum_v.tile([P, GROUP, D], F32, name="v_bank")
        nc.tensor.matmul(out=gain_bank[:, 0, :], lhsT=all_ones[:], rhs=gain_rows[:], start=True, stop=True)
        nc.tensor.matmul(out=gain_bank[:, 1, 0:HALF], lhsT=all_ones[:], rhs=gain_rows[:, HALF:D], start=True, stop=True)
        nc.tensor.matmul(out=gain_bank[:, 1, HALF:D], lhsT=minus_ones[:], rhs=gain_rows[:, 0:HALF], start=True, stop=True)

        x_of_pair = []

        def load_group(g):
            b, first = g // GROUPS_PER_BATCH, GROUP * (g % GROUPS_PER_BATCH)
            pieces = (PAIR, PAIR) if g == 0 else (GROUP,)
            for width in pieces:
                x_in = x_pool.tile([P, width, C], BF16, name="x_in")
                nc.sync.dma_start(out=x_in[:], in_=x_by_slot[b, :, first : first + width, :])
                for s in range(0, width, PAIR):
                    x_of_pair.append((x_in, s))
                first += width

        load_group(0)
        load_group(1)
        nc.sync.dma_start(out=w_words[:].bitcast(I32), in_=W_qkv_words[0].bitcast(I32))
        for quadrant in range(4):
            nc.sync.dma_start(
                out=w_scales[32 * quadrant : 32 * quadrant + 4, :].bitcast(I32),
                in_=W_qkv_scales[0, 4 * quadrant : 4 * quadrant + 4, :].bitcast(I32),
            )
        for g in range(2, AHEAD):
            load_group(g)

        fine = const.tile([P, ROOT], F32)
        coarse = const.tile([P, ROOT], F32)
        nc.vector.tensor_scalar_mul(out=fine[:, 0:1], in0=one[:], scalar1=1.0 / (2.0 * math.pi))
        nc.vector.tensor_copy(out=coarse[:, 0:1], in_=one[:])
        filled = 1
        while filled < ROOT:
            for sequence, step in ((fine, 1), (coarse, ROOT)):
                nc.vector.tensor_scalar_mul(
                    out=sequence[:, filled : 2 * filled],
                    in0=sequence[:, 0:filled],
                    scalar1=ROPE_BASE ** (-filled * step / HALF),
                )
            filled *= 2
        token = const.tile([P, SLOTS], F32)
        nc.vector.tensor_copy(out=token[:], in_=token_int[:])
        turns_per_token = const.tile([P, HALF], F32)
        nc.vector.tensor_tensor(
            out=turns_per_token[:].rearrange("p (j i) -> p j i", i=ROOT),
            in0=coarse[:].unsqueeze(2).to_broadcast([P, ROOT, ROOT]),
            in1=fine[:].unsqueeze(1).to_broadcast([P, ROOT, ROOT]),
            op=ALU.mult,
        )

        trig = const.tile([P, SLOTS, 2, HALF], F32)
        for first in range(0, SLOTS, 2 * GROUP):
            both = (slice(first, first + GROUP), slice(first + GROUP, first + 2 * GROUP))
            turns, whole, part, size = [], [], [], []
            for slots in both:
                turns.append(angle_pool.tile([P, GROUP, HALF], F32, name="turns"))
                nc.vector.tensor_tensor(
                    out=turns[-1][:],
                    in0=token[:, slots].unsqueeze(2).to_broadcast([P, GROUP, HALF]),
                    in1=turns_per_token[:].unsqueeze(1).to_broadcast([P, GROUP, HALF]),
                    op=ALU.mult,
                )
            for i in range(2):
                whole.append(angle_pool.tile([P, GROUP, HALF], F32, name="whole"))
                nc.vector.tensor_scalar(
                    out=whole[i][:],
                    in0=turns[i][:],
                    scalar1=ROUND_MAGIC,
                    scalar2=ROUND_MAGIC,
                    op0=ALU.add,
                    op1=ALU.subtract,
                )
            for i in range(2):
                part.append(angle_pool.tile([P, GROUP, HALF], F32, name="part"))
                nc.vector.tensor_tensor(out=part[i][:], in0=turns[i][:], in1=whole[i][:], op=ALU.subtract)
            for i in range(2):
                nc.scalar.activation(out=trig[:, both[i], 1, :], in_=part[i][:], func=ACT.Sin, scale=2.0 * math.pi)
                size.append(angle_pool.tile([P, GROUP, HALF], F32, name="size"))
                nc.scalar.activation(out=size[i][:], in_=part[i][:], func=ACT.Abs)
            for i in range(2):
                nc.scalar.activation(
                    out=trig[:, both[i], 0, :], in_=size[i][:], func=ACT.Sin, scale=-2.0 * math.pi, bias=math.pi / 2.0
                )
        nc.scalar.activation(out=scratch[:, 1:2], in_=one[:], func=ACT.Abs_reciprocal_sqrt)

        gains = const.tile([P, 2, D], F32)
        nc.vector.tensor_copy(out=gains[:], in_=gain_bank[:, 0:2, :])
        table = const.tile([P, SLOTS, 2, D], F32)

        def build_table(engine, block, gain_pair):
            slots = slice(block * GROUP, (block + 1) * GROUP)
            for a in range(2):
                engine.tensor_tensor(
                    out=table[:, slots, a, :].rearrange("p s (j c) -> p s j c", j=2),
                    in0=trig[:, slots, a, :].unsqueeze(2).to_broadcast([P, GROUP, 2, HALF]),
                    in1=gain_pair[:, a, :].rearrange("p (j c) -> p j c", j=2).unsqueeze(1).to_broadcast(
                        [P, GROUP, 2, HALF]
                    ),
                    op=ALU.mult,
                )

        for block in range(1, GROUPS_PER_BATCH):
            build_table(nc.gpsimd, block, gains)

        def transpose_pair(n):
            x_in, first = x_of_pair[n]
            words_in = x_in[:].bitcast(F32)
            xt = psum_xt.tile([P, PAIR, 2, P], F32, name="xt")
            for s in range(PAIR):
                for u in range(2):
                    nc.tensor.transpose(xt[:, s, u, :], words_in[:, first + s, u : C // 2 : 2], ident[:])
            return xt

        def on_vector(n):
            return n < HEAD_PAIRS

        def copy_pair(n, xt, grouped):
            half = n % 2
            out = grouped[:, half * PAIR * C : (half + 1) * PAIR * C].bitcast(F32)
            out = out.rearrange("p (s r u) -> p s r u", s=PAIR, u=2)
            if on_vector(n):
                nc.vector.tensor_copy(out=out, in_=xt[:].rearrange("p s u r -> p s r u"))
            else:
                nc.scalar.copy(out=out, in_=xt[:].rearrange("p s u r -> p s r u"))

        def quantise_group(grouped):
            x_words = quant_pool.tile([P, GROUP * P], U32, align_bytes=64, name="x_words")
            x_scales = quant_pool.tile([P, GROUP * P], U8, align_bytes=64, name="x_scales")
            nc.vector.quantize_mx(out=x_words[:].bitcast(FP8X4), scales=x_scales[:], in_=grouped[:])
            return x_words, x_scales

        def multiply_pair(n, x_words, x_scales, v_bank):
            half = n % 2
            qk_bank = psum_qk.tile([P, PAIR, 2 * D], F32, name="qk_bank")
            for s in range(PAIR):
                slot = half * PAIR + s
                tokens = slice(slot * P, (slot + 1) * P)
                nc.tensor.matmul_mx(
                    out=qk_bank[:, s, :],
                    lhsT=x_words[:, tokens].bitcast(FP8X4),
                    lhsT_scale=x_scales[:, tokens],
                    rhs=w_words[:, 0 : 2 * 2 * D].bitcast(FP4X4),
                    rhs_scale=w_scales[:, 0 : 2 * D],
                    start=True,
                    stop=True,
                )
                width = min(2, GROUP - slot)
                end = GROUP - slot
                nc.tensor.matmul_mx(
                    out=v_bank[:, end - width : end, :].rearrange("p s d -> p (s d)"),
                    lhsT=x_words[:, tokens].bitcast(FP8X4),
                    lhsT_scale=x_scales[:, tokens],
                    rhs=w_words[:, 2 * (3 - width) * D : 2 * 3 * D].bitcast(FP4X4),
                    rhs_scale=w_scales[:, (3 - width) * D : 3 * D],
                    start=True,
                    stop=True,
                )
            return qk_bank

        def squares_pair(n, qk_bank, sum_squares):
            half = n % 2
            for s in range(PAIR):
                for o in range(2):
                    column = 2 * (half * PAIR + s) + o
                    squares = norm_pool.tile([P, D], F32, name="squares")
                    nc.scalar.activation(
                        out=squares[:],
                        in_=qk_bank[:, s, o * D : (o + 1) * D],
                        func=ACT.Square,
                        accum_out=sum_squares[:, column : column + 1],
                    )

        def rotate_pair(n, qk_bank, inv_norm, products):
            half = n % 2
            first_slot = PAIR * (n % (SLOTS // PAIR))
            for s in range(PAIR):
                slot = half * PAIR + s
                for o in range(2):
                    nc.vector.scalar_tensor_tensor(
                        out=products[:, :, o, slot, :],
                        in0=qk_bank[:, s, o * D : (o + 1) * D].unsqueeze(1).to_broadcast([P, 2, D]),
                        scalar=inv_norm[:, 2 * slot + o : 2 * slot + o + 1],
                        in1=table[:, first_slot + s, :, :],
                        op0=ALU.mult,
                        op1=ALU.mult,
                    )

        def place(g):
            return g // GROUPS_PER_BATCH, GROUP * (g % GROUPS_PER_BATCH)

        xts, groupeds, codes, v_banks, qk_banks = [], [], [], [], []
        sums, inv_norms, prods, v_outs = [], [], [], []
        for r in range(N_PAIRS + 10):
            if r == 4:
                build_table(nc.vector, 0, gain_bank)
            if r % 2 == 1 and 0 <= (r - 3) // 2 < N_GROUPS:
                codes.append(quantise_group(groupeds[(r - 3) // 2]))
            if 0 <= r - 1 < N_PAIRS:
                if (r - 1) % 2 == 0:
                    grouped = quant_pool.tile([P, GROUP * C], BF16, align_bytes=64, name="grouped")
                    groupeds.append(grouped)
                copy_pair(r - 1, xts[r - 1], groupeds[(r - 1) // 2])
            if r % 2 == 0:
                if 0 <= r - 4 < N_PAIRS:
                    g = (r - 4) // 2
                    v_bank = psum_v.tile([P, GROUP, D], F32, name="v_bank")
                    v_banks.append(v_bank)
                for i in range(2):
                    if r + i < N_PAIRS and r != 4:
                        xts.append(transpose_pair(r + i))
                    if 0 <= r - 4 < N_PAIRS:
                        qk_banks.append(multiply_pair(r - 4 + i, codes[g][0], codes[g][1], v_bank))
                if r == 4:
                    for n in (r, r + 1):
                        xts.append(transpose_pair(n))
            if 0 <= r - 5 < N_PAIRS:
                n = r - 5
                g = n // 2
                if n % 2 == 0:
                    sum_squares = norm_pool.tile([P, GROUP * 2], F32, name="sum_squares")
                    sums.append(sum_squares)
                squares_pair(n, qk_banks[n], sums[g])
                if g == N_GROUPS - 1:
                    if n % 2 == 0:
                        inv_norm = norm_pool.tile([P, GROUP * 2], F32, name="inv_norm")
                        inv_norms.append(inv_norm)
                    mine = slice((n % 2) * GROUP, (n % 2 + 1) * GROUP)
                    nc.scalar.activation(
                        out=inv_norms[g][:, mine], in_=sums[g][:, mine], func=ACT.Abs_reciprocal_sqrt
                    )
                if n % 2 == 1:
                    v_out = out_pool.tile([P, GROUP, D], F32, name="v_out")
                    v_outs.append(v_out)
                    nc.scalar.copy(out=v_out[:], in_=v_banks[g][:, ::-1, :])
                    if g < N_GROUPS - 1:
                        inv_norm = norm_pool.tile([P, GROUP * 2], F32, name="inv_norm")
                        nc.scalar.activation(out=inv_norm[:], in_=sums[g][:], func=ACT.Abs_reciprocal_sqrt)
                        inv_norms.append(inv_norm)
                    b, first_slot = place(g)
                    nc.sync.dma_start(out=v_by_slot[b, :, first_slot : first_slot + GROUP, :], in_=v_out[:])
            if 0 <= r - 7 < N_PAIRS:
                n = r - 7
                if n % 2 == 0:
                    products = prod_pool.tile([P, 2, 2, GROUP, D], F32, name="products")
                    prods.append(products)
                rotate_pair(n, qk_banks[n], inv_norms[n // 2], prods[n // 2])
            if N_PAIRS - 4 <= r - 8 < N_PAIRS:
                half = (r - 8) % 2
                g = (r - 8) // 2
                engine = nc.vector if g == N_GROUPS - 1 or half == 0 else nc.gpsimd
                if half == 0:
                    last_out = out_pool.tile([P, 2, GROUP, D], F32, name="qk_out")
                mine = slice(half * PAIR, (half + 1) * PAIR)
                for o in range(2):
                    terms = prods[g][:, :, o, mine, :].rearrange("p a s (h c) -> p a s h c", h=2)
                    engine.tensor_tensor(
                        out=last_out[:, o, mine, :].rearrange("p s (h c) -> p s h c", h=2),
                        in0=terms[:, 0],
                        in1=terms[:, 1, :, ::-1, :],
                        op=ALU.add,
                    )
                b, first_slot = place(g)
                slots = slice(first_slot + half * PAIR, first_slot + (half + 1) * PAIR)
                nc.sync.dma_start(out=q_by_slot[b, :, slots, :], in_=last_out[:, 0, mine, :])
                nc.sync.dma_start(out=k_by_slot[b, :, slots, :], in_=last_out[:, 1, mine, :])
            if r % 2 == 1 and 0 <= (r - 9) // 2 < N_GROUPS - 2:
                g = (r - 9) // 2
                qk_out = out_pool.tile([P, 2, GROUP, D], F32, name="qk_out")
                terms = prods[g][:].rearrange("p a o s (h c) -> p a (o s) h c", h=2)
                nc.gpsimd.tensor_tensor(
                    out=qk_out[:].rearrange("p o s (h c) -> p (o s) h c", h=2),
                    in0=terms[:, 0],
                    in1=terms[:, 1, :, ::-1, :],
                    op=ALU.add,
                )
                b, first_slot = place(g)
                slots = slice(first_slot, first_slot + GROUP)
                nc.sync.dma_start(out=q_by_slot[b, :, slots, :], in_=qk_out[:, 0])
                nc.sync.dma_start(out=k_by_slot[b, :, slots, :], in_=qk_out[:, 1])
                if g + AHEAD < N_GROUPS:
                    load_group(g + AHEAD)
